import numpy as np
import ml_dtypes


def mxq(x, axis, fmt="e4m3"):
    dtype, down = {"e4m3": (ml_dtypes.float8_e4m3fn, 7), "e5m2": (ml_dtypes.float8_e5m2, 14)}[fmt]
    v = np.moveaxis(np.asarray(x, np.float32).astype(ml_dtypes.bfloat16).astype(np.float64), axis, -1)
    blocks = v.reshape(v.shape[:-1] + (-1, 32))
    amax = np.abs(blocks).max(-1, keepdims=True)
    byte = np.maximum(np.where(amax > 0, np.frexp(amax)[1] - 1 + 127, 0) - down, 1)
    scale = np.exp2(byte - 127.0)
    codes = (blocks / scale).astype(np.float32).astype(dtype).astype(np.float64)
    return np.moveaxis((codes * scale).reshape(v.shape), -1, axis)


WIDE = False


def mx_kscale(k):
    if not WIDE:
        return np.ones(k)
    levels = np.array([10, -10, 5, -5, 0])
    a = np.random.permutation(np.resize(levels, k // 512 * 4)).reshape(k // 512, 4)
    idx = np.arange(k)
    return np.exp2(a[idx // 512, idx % 128 // 32])


BF16 = ml_dtypes.bfloat16


def bf(x):
    return np.asarray(x, np.float32).astype(BF16)


def f64(x):
    return np.asarray(x).astype(np.float64)


B, N, D, F = 4, 64, 512, 128


def setup_inputs():
    s, t = mx_kscale(D), mx_kscale(D)
    sst = np.concatenate([s, s, t])
    return {
        'node_h': bf(np.random.standard_normal((B, N, D)) * 0.5 * s),
        'rel_h': bf(np.random.standard_normal((B, N, N, D)) * 0.6 * t),
        'W_go': bf(np.random.standard_normal((D, D)) / np.sqrt(D) / s[:, None]),
        'b_go': bf(np.random.standard_normal(D) * 0.3),
        'W_gr': bf(np.random.standard_normal((3 * D, D)) * 1.5 / np.sqrt(3 * D) / sst[:, None]),
        'b_gr': bf(np.random.standard_normal(D) * 0.3),
        'W_esa': bf(np.random.standard_normal((D, F)) * 1.5 / np.sqrt(D)),
        'b_esa': bf(np.random.standard_normal(F) * 0.3),
    }


def reference(node_h, rel_h, W_go, b_go, W_gr, b_gr, W_esa, b_esa):
    xq = mxq(f64(node_h), 2, 'e4m3')
    wg = f64(W_gr)
    new_x = np.tanh((xq @ mxq(f64(W_go), 0, 'e4m3')) + f64(b_go))
    pre = ((xq @ mxq(wg[:D], 0, 'e4m3'))[:, :, None, :]
           + (xq @ mxq(wg[D:2 * D], 0, 'e4m3'))[:, None, :, :]
           + (mxq(f64(rel_h), 3, 'e4m3') @ mxq(wg[2 * D:], 0, 'e4m3')) + f64(b_gr))
    rel = np.tanh(pre)
    e = (mxq(rel, 3, 'e4m3') @ mxq(f64(W_esa), 0, 'e4m3')) + f64(b_esa)
    p = np.exp(e - e.max(axis=1, keepdims=True))
    attn = p / p.sum(axis=1, keepdims=True)
    return new_x, (attn * e).sum(axis=2)

@@ -1,0 +1,312 @@
+from contextlib import ExitStack
+
+import concourse.bass as bass
+import concourse.mybir as mybir
+import concourse.tile as tile
+from concourse.masks import make_identity
+
+F32 = mybir.dt.float32
+BF16 = mybir.dt.bfloat16
+U32 = mybir.dt.uint32
+U8 = mybir.dt.uint8
+FP8X4 = mybir.dt.float8_e4m3fn_x4
+ACTF = mybir.ActivationFunctionType
+ALU = mybir.AluOpType
+AX = mybir.AxisListType
+
+P = 128
+B, N, D, F = 4, 64, 512, 128
+FLOPS = 2 * (3 * B * N * D * D + B * N * N * D * D + B * N * N * D * F)
+
+TILES_PER_B = 8
+CHUNKS = 4
+TANH_SPLIT = 2
+
+
+def tile_languagemsgencoder_pb_t_kernel(
+    tc, node_h, rel_h, W_go, b_go, W_gr, b_gr, W_esa, b_esa, out_0, out_1
+):
+    nc = tc.nc
+    with ExitStack() as ctx:
+        const = ctx.enter_context(tc.tile_pool(name="const", bufs=1))
+        wtmp = ctx.enter_context(tc.tile_pool(name="wtmp", bufs=2))
+        rawp = ctx.enter_context(tc.tile_pool(name="rawp", bufs=4))
+        work = ctx.enter_context(tc.tile_pool(name="work", bufs=3))
+        small = ctx.enter_context(tc.tile_pool(name="small", bufs=4))
+        ps_tr = ctx.enter_context(tc.psum_pool(name="ps_tr", bufs=2))
+        ps_p = ctx.enter_context(tc.psum_pool(name="ps_p", bufs=4))
+        ps_e = ctx.enter_context(tc.psum_pool(name="ps_e", bufs=2))
+
+        ident = const.tile([P, P], F32, name="ident")
+        make_identity(nc, ident[:])
+
+        def load_k_first(rows, name):
+            raw = const.tile([P, 4, D], BF16, name=name)
+            nc.sync.dma_start(
+                out=raw[:].rearrange("p (u e) c -> p u (e c)", u=2),
+                in_=rows.rearrange("(u q e) c -> q u (e c)", u=2, e=2),
+            )
+            return raw
+
+        rel_rows = rel_h.rearrange("b i j k -> b (i j) k")
+        raw_chunks = {}
+
+        def load_chunk(c):
+            b, h = divmod(c, 4)
+            raw = rawp.tile([P, 8, D], BF16, name="raw", tag="raw")
+            nc.sync.dma_start(
+                out=raw[:],
+                in_=rel_rows[b].rearrange("(p n) k -> p n k", n=32)[:, 8 * h : 8 * h + 8, :],
+            )
+            raw_chunks[c] = raw
+
+        gc_raw = load_k_first(W_gr[2 * D : 3 * D, :], "gc_raw")
+        x_raw = const.tile([P, 2, D], BF16, name="x_raw")
+        nc.sync.dma_start(
+            out=x_raw[:], in_=node_h.rearrange("b n k -> (b n) k").rearrange("(r p) k -> p r k", p=P)
+        )
+        load_chunk(0)
+        ga_raw = load_k_first(W_gr[0:D, :], "ga_raw")
+        gb_raw = load_k_first(W_gr[D : 2 * D, :], "gb_raw")
+
+        bgr_bf = const.tile([P, 4], BF16, name="bgr_bf")
+        besa_bf = const.tile([P, 1], BF16, name="besa_bf")
+        we_raw = const.tile([P, 4, F], BF16, name="we_raw")
+        with nc.allow_non_contiguous_dma(reason="small per-partition bias loads"):
+            nc.scalar.dma_start(out=bgr_bf[:], in_=b_gr.rearrange("(p t) -> p t", t=4))
+            nc.scalar.dma_start(out=besa_bf[:], in_=b_esa.rearrange("(p t) -> p t", t=1))
+        nc.scalar.dma_start(out=we_raw[:], in_=W_esa.rearrange("(p t) n -> p t n", t=4))
+        load_chunk(1)
+        go_raw = load_k_first(W_go, "go_raw")
+        bgo_bc = const.tile([P, D], BF16, name="bgo_bc")
+        nc.sync.dma_start(out=bgo_bc[:], in_=b_go.partition_broadcast(P))
+
+        def quantise(grouped_flat, width, name):
+            codes = const.tile([P, width], U32, name=name + "_c", align_bytes=64)
+            plane = const.tile([P, width], U8, name=name + "_s", align_bytes=64)
+            nc.vector.quantize_mx(out=codes[:].bitcast(FP8X4), scales=plane[:], in_=grouped_flat)
+            return codes, plane
+
+        def stationary(raw, name):
+            grp = wtmp.tile([P, 4, P, 4], BF16, name="grp", tag="grp", align_bytes=64)
+            src = raw[:].rearrange("p t (pp tm) -> p tm pp t", tm=4)
+            nc.vector.tensor_copy(out=grp[:, 0:2], in_=src[:, 0:2])
+            nc.scalar.copy(out=grp[:, 2:4], in_=src[:, 2:4])
+            return quantise(grp[:].rearrange("p a b c -> p (a b c)"), D, name)
+
+        gc_c, gc_s = stationary(gc_raw, "gc")
+
+        x_tr = ps_tr.tile([P, 2, 2, P], F32, name="x_tr", tag="tr")
+        for r in range(2):
+            xw = x_raw[:, r, :].bitcast(F32)
+            for u in range(2):
+                nc.tensor.transpose(x_tr[:, r, u, :], xw[:, P * u : P * u + P], ident[:])
+        xg = const.tile([P, 4 * B * N], BF16, name="xg", align_bytes=64)
+        xgw = xg[:].bitcast(F32)
+        nc.vector.tensor_copy(
+            out=xgw.rearrange("p (r c u) -> p r c u", r=2, u=2),
+            in_=x_tr[:].rearrange("p r u c -> p r c u"),
+        )
+        xrep = const.tile([P, 4 * B * 2 * N], BF16, name="xrep", align_bytes=64)
+        nc.vector.tensor_copy(
+            out=xrep[:].bitcast(F32).rearrange("p (b r w) -> p b r w", b=B, r=2),
+            in_=xgw.rearrange("p (b w) -> p b w", b=B).unsqueeze(2).to_broadcast([P, B, 2, 2 * N]),
+        )
+        x_c, x_s = quantise(xg[:], B * N, "x")
+        xr_c, xr_s = quantise(xrep[:], B * 2 * N, "xr")
+
+        ga_c, ga_s = stationary(ga_raw, "ga")
+        gb_c, gb_s = stationary(gb_raw, "gb")
+
+        bgr = const.tile([P, 4], F32, name="bgr")
+        nc.vector.tensor_copy(out=bgr[:], in_=bgr_bf[:])
+        besa = const.tile([P, 1], F32, name="besa")
+        nc.vector.tensor_copy(out=besa[:], in_=besa_bf[:])
+
+        bb = const.tile([P, B * N, 4], F32, name="bb")
+        for h in range(2):
+            pb = ps_p.tile([P, 4, P], F32, name="pb", tag="pp")
+            for tm in range(4):
+                nc.tensor.matmul_mx(
+                    out=pb[:, tm, :],
+                    lhsT=gb_c[:, P * tm : P * tm + P].bitcast(FP8X4),
+                    lhsT_scale=gb_s[:, P * tm : P * tm + P],
+                    rhs=x_c[:, P * h : P * h + P].bitcast(FP8X4),
+                    rhs_scale=x_s[:, P * h : P * h + P],
+                    start=True,
+                    stop=True,
+                )
+            nc.vector.tensor_tensor(
+                out=bb[:, P * h : P * h + P, :],
+                in0=pb[:].rearrange("p t c -> p c t"),
+                in1=bgr[:].unsqueeze(1).to_broadcast([P, P, 4]),
+                op=ALU.add,
+            )
+        bb_v = bb[:].rearrange("p (b jh n) t -> p b jh n t", b=B, jh=2)
+
+        we_grp = const.tile([P, F, 4], BF16, name="we_grp", align_bytes=64)
+        nc.vector.tensor_copy(out=we_grp[:], in_=we_raw[:].rearrange("p t n -> p n t"))
+        we_c, we_s = quantise(we_grp[:].rearrange("p n t -> p (n t)"), F, "we")
+
+        acc8 = const.tile([P, B, 8, N], F32, name="acc8")
+        osum = const.tile([P, B * N], F32, name="osum")
+
+        def new_x():
+            go_grp = wtmp.tile([P, D, 4], BF16, name="go_grp", tag="grp", align_bytes=64)
+            nc.vector.tensor_copy(out=go_grp[:], in_=go_raw[:].rearrange("p t c -> p c t"))
+            go_c, go_s = quantise(go_grp[:].rearrange("p c t -> p (c t)"), D, "go")
+            out_rows = out_0.rearrange("b n d -> (b n) d")
+            for r in range(2):
+                px = ps_e.tile([P, D], F32, name="px", tag="pe")
+                nc.tensor.matmul_mx(
+                    out=px[:],
+                    lhsT=x_c[:, P * r : P * r + P].bitcast(FP8X4),
+                    lhsT_scale=x_s[:, P * r : P * r + P],
+                    rhs=go_c[:].bitcast(FP8X4),
+                    rhs_scale=go_s[:],
+                    start=True,
+                    stop=True,
+                )
+                nx = work.tile([P, D], F32, name="nx", tag="pq")
+                nc.vector.tensor_tensor(out=nx[:], in0=px[:], in1=bgo_bc[:], op=ALU.add)
+                nxt = work.tile([P, D], F32, name="nxt", tag="pq")
+                nc.scalar.activation(out=nxt[:], in_=nx[:], func=ACTF.Tanh)
+                nc.sync.dma_start(out=out_rows[P * r : P * r + P, :], in_=nxt[:])
+
+        def finish_pair(h):
+            for b in (2 * h, 2 * h + 1):
+                nc.vector.tensor_reduce(
+                    out=osum[:, N * b : N * b + N],
+                    in_=acc8[:, b].rearrange("p j i -> p i j"),
+                    axis=AX.X,
+                    op=ALU.add,
+                )
+            pf = ps_e.tile([P, D], F32, name="pf", tag="pe")
+            nc.tensor.transpose(pf[:, 0:P], osum[:, P * h : P * h + P], ident[:])
+            ot = work.tile([P, P], F32, name="ot", tag="ot")
+            nc.vector.tensor_copy(out=ot[:], in_=pf[:, 0:P])
+            nc.sync.dma_start(
+                out=out_1.rearrange("b i c -> (b i) c")[P * h : P * h + P, :], in_=ot[:]
+            )
+
+        n_tiles = B * TILES_PER_B
+        for T in range(n_tiles):
+            b, g = divmod(T, TILES_PER_B)
+            c, half = divmod(T, 2)
+            if half == 0 and c + 2 < n_tiles // 2:
+                load_chunk(c + 2)
+            raw = raw_chunks[c]
+
+            g1 = work.tile([P, 4 * D], BF16, name="g1", tag="g1", align_bytes=64)
+            g1w = g1[:].bitcast(F32).rearrange("p (c jh i u) -> p c jh i u", c=CHUNKS, jh=2, u=2)
+            for pair in range(2):
+                tr = ps_tr.tile([P, 2, 2, P], F32, name="tr", tag="tr")
+                for k in range(2):
+                    rw = raw[:, 4 * half + 2 * pair + k, :].bitcast(F32)
+                    for u in range(2):
+                        nc.tensor.transpose(tr[:, k, u, :], rw[:, P * u : P * u + P], ident[:])
+                for k in range(2):
+                    nc.scalar.copy(
+                        out=g1w[:, 2 * pair + k],
+                        in_=tr[:, k].rearrange("p u (i jh) -> p jh i u", jh=2),
+                    )
+            c1 = work.tile([P, D], U32, name="c1", tag="c1", align_bytes=64)
+            s1 = work.tile([P, D], U8, name="s1", tag="s1", align_bytes=64)
+            nc.vector.quantize_mx(out=c1[:].bitcast(FP8X4), scales=s1[:], in_=g1[:])
+
+            a32 = work.tile([P, 4 * D], F32, name="a32", tag="a32")
+            for ci in range(CHUNKS):
+                n = CHUNKS * g + ci
+                pp = ps_p.tile([P, 4, P], F32, name="pp", tag="pp")
+                for tm in range(4):
+                    nc.tensor.matmul_mx(
+                        out=pp[:, tm, :],
+                        lhsT=gc_c[:, P * tm : P * tm + P].bitcast(FP8X4),
+                        lhsT_scale=gc_s[:, P * tm : P * tm + P],
+                        rhs=c1[:, P * ci : P * ci + P].bitcast(FP8X4),
+                        rhs_scale=s1[:, P * ci : P * ci + P],
+                        start=True,
+                        stop=False,
+                    )
+                    nc.tensor.matmul_mx(
+                        out=pp[:, tm, :],
+                        lhsT=ga_c[:, P * tm : P * tm + P].bitcast(FP8X4),
+                        lhsT_scale=ga_s[:, P * tm : P * tm + P],
+                        rhs=xr_c[:, P * b : P * b + P].bitcast(FP8X4),
+                        rhs_scale=xr_s[:, P * b : P * b + P],
+                        start=False,
+                        stop=True,
+                    )
+                nc.vector.tensor_tensor(
+                    out=a32[:, D * ci : D * ci + D].rearrange("p (jh i t) -> p jh i t", jh=2, t=4),
+                    in0=pp[:].rearrange("p t (jh i) -> p jh i t", jh=2),
+                    in1=bb_v[:, b, :, n, :].unsqueeze(2).to_broadcast([P, 2, N, 4]),
+                    op=ALU.add,
+                )
+            g2 = work.tile([P, 4 * D], BF16, name="g2", tag="g2", align_bytes=64)
+            w = 4 * D // TANH_SPLIT
+            for s in range(TANH_SPLIT):
+                nc.scalar.activation(
+                    out=g2[:, w * s : w * s + w], in_=a32[:, w * s : w * s + w], func=ACTF.Tanh
+                )
+            c2 = work.tile([P, D], U32, name="c2", tag="c2", align_bytes=64)
+            s2 = work.tile([P, D], U8, name="s2", tag="s2", align_bytes=64)
+            nc.vector.quantize_mx(out=c2[:].bitcast(FP8X4), scales=s2[:], in_=g2[:])
+
+            pe = ps_e.tile([P, D], F32, name="pe", tag="pe")
+            nc.tensor.matmul_mx(
+                out=pe[:],
+                lhsT=we_c[:].bitcast(FP8X4),
+                lhsT_scale=we_s[:],
+                rhs=c2[:].bitcast(FP8X4),
+                rhs_scale=s2[:],
+                start=True,
+                stop=True,
+            )
+            negmax = small.tile([P, 8], F32, name="negmax", tag="negmax")
+            nc.vector.tensor_reduce(
+                out=negmax[:],
+                in_=pe[:].rearrange("p (j i) -> p j i", j=8),
+                axis=AX.X,
+                op=ALU.max,
+                negate=True,
+            )
+            pexp = work.tile([P, D], F32, name="pexp", tag="pexp")
+            ssum = small.tile([P, 8], F32, name="ssum", tag="ssum")
+            for j in range(8):
+                nc.scalar.activation(
+                    out=pexp[:, N * j : N * j + N],
+                    in_=pe[:, N * j : N * j + N],
+                    func=ACTF.Exp,
+                    bias=negmax[:, j : j + 1],
+                    scale=1.0,
+                    accum_out=ssum[:, j : j + 1],
+                )
+            rinv = small.tile([P, 8], F32, name="rinv", tag="rinv")
+            nc.vector.reciprocal(out=rinv[:], in_=ssum[:])
+            q = work.tile([P, D], F32, name="q", tag="pq")
+            nc.vector.scalar_tensor_tensor(
+                out=q[:], in0=pe[:], scalar=besa[:, 0:1], in1=pexp[:], op0=ALU.add, op1=ALU.mult
+            )
+            for j in range(8):
+                if g == 0:
+                    nc.vector.tensor_scalar(
+                        out=acc8[:, b, j, :],
+                        in0=q[:, N * j : N * j + N],
+                        scalar1=rinv[:, j : j + 1],
+                        scalar2=None,
+                        op0=ALU.mult,
+                    )
+                else:
+                    nc.vector.scalar_tensor_tensor(
+                        out=acc8[:, b, j, :],
+                        in0=q[:, N * j : N * j + N],
+                        scalar=rinv[:, j : j + 1],
+                        in1=acc8[:, b, j, :],
+                        op0=ALU.mult,
+                        op1=ALU.add,
+                    )
+            if T == 1:
+                new_x()
+            if g == TILES_PER_B - 1 and b % 2 == 1:
+                finish_pair(b // 2)

@@ -1,8 +1,6 @@
 from contextlib import ExitStack
 
-import concourse.bass as bass
 import concourse.mybir as mybir
-import concourse.tile as tile
 from concourse.masks import make_identity
 
 F32 = mybir.dt.float32
@@ -19,8 +17,10 @@ B, N, D, F = 4, 64, 512, 128
 FLOPS = 2 * (3 * B * N * D * D + B * N * N * D * D + B * N * N * D * F)
 
 TILES_PER_B = 8
+N_TILES = B * TILES_PER_B
 CHUNKS = 4
 TANH_SPLIT = 2
+GPS_TILES = N_TILES - 1
 
 
 def tile_languagemsgencoder_pb_t_kernel(
@@ -28,6 +28,7 @@ def tile_languagemsgencoder_pb_t_kernel(
 ):
     nc = tc.nc
     with ExitStack() as ctx:
+        ctx.enter_context(tc.manual_schedule())
         const = ctx.enter_context(tc.tile_pool(name="const", bufs=1))
         wtmp = ctx.enter_context(tc.tile_pool(name="wtmp", bufs=2))
         rawp = ctx.enter_context(tc.tile_pool(name="rawp", bufs=4))
@@ -51,23 +52,17 @@ def tile_languagemsgencoder_pb_t_kernel(
         rel_rows = rel_h.rearrange("b i j k -> b (i j) k")
         raw_chunks = {}
 
-        def load_chunk(c):
+        def load_chunk(c, pieces=1):
             b, h = divmod(c, 4)
             raw = rawp.tile([P, 8, D], BF16, name="raw", tag="raw")
-            nc.sync.dma_start(
-                out=raw[:],
-                in_=rel_rows[b].rearrange("(p n) k -> p n k", n=32)[:, 8 * h : 8 * h + 8, :],
-            )
+            src = rel_rows[b].rearrange("(p n) k -> p n k", n=32)
+            step = 8 // pieces
+            for s in range(pieces):
+                nc.sync.dma_start(
+                    out=raw[:, step * s : step * s + step, :],
+                    in_=src[:, 8 * h + step * s : 8 * h + step * s + step, :],
+                )
             raw_chunks[c] = raw
-
-        gc_raw = load_k_first(W_gr[2 * D : 3 * D, :], "gc_raw")
-        x_raw = const.tile([P, 2, D], BF16, name="x_raw")
-        nc.sync.dma_start(
-            out=x_raw[:], in_=node_h.rearrange("b n k -> (b n) k").rearrange("(r p) k -> p r k", p=P)
-        )
-        load_chunk(0)
-        ga_raw = load_k_first(W_gr[0:D, :], "ga_raw")
-        gb_raw = load_k_first(W_gr[D : 2 * D, :], "gb_raw")
 
         bgr_bf = const.tile([P, 4], BF16, name="bgr_bf")
         besa_bf = const.tile([P, 1], BF16, name="besa_bf")
@@ -75,8 +70,19 @@ def tile_languagemsgencoder_pb_t_kernel(
         with nc.allow_non_contiguous_dma(reason="small per-partition bias loads"):
             nc.scalar.dma_start(out=bgr_bf[:], in_=b_gr.rearrange("(p t) -> p t", t=4))
             nc.scalar.dma_start(out=besa_bf[:], in_=b_esa.rearrange("(p t) -> p t", t=1))
-        nc.scalar.dma_start(out=we_raw[:], in_=W_esa.rearrange("(p t) n -> p t n", t=4))
+
+        x_raw = const.tile([P, 2, D], BF16, name="x_raw")
+        nc.sync.dma_start(
+            out=x_raw[:], in_=node_h.rearrange("b n k -> (b n) k").rearrange("(r p) k -> p r k", p=P)
+        )
+        gb_raw = load_k_first(W_gr[D : 2 * D, :], "gb_raw")
+        gc_raw = load_k_first(W_gr[2 * D : 3 * D, :], "gc_raw")
+        load_chunk(0, pieces=2)
+        ga_raw = load_k_first(W_gr[0:D, :], "ga_raw")
         load_chunk(1)
+        nc.sync.dma_start(out=we_raw[:], in_=W_esa.rearrange("(p t) n -> p t n", t=4))
+        load_chunk(2)
+        load_chunk(3)
         go_raw = load_k_first(W_go, "go_raw")
         bgo_bc = const.tile([P, D], BF16, name="bgo_bc")
         nc.sync.dma_start(out=bgo_bc[:], in_=b_go.partition_broadcast(P))
@@ -87,14 +93,197 @@ def tile_languagemsgencoder_pb_t_kernel(
             nc.vector.quantize_mx(out=codes[:].bitcast(FP8X4), scales=plane[:], in_=grouped_flat)
             return codes, plane
 
-        def stationary(raw, name):
-            grp = wtmp.tile([P, 4, P, 4], BF16, name="grp", tag="grp", align_bytes=64)
+        def regroup_stationary(raw):
+            grp = wtmp.tile([P, 4, P, 4], BF16, name="grp", tag="grp", bufs=3, align_bytes=64)
             src = raw[:].rearrange("p t (pp tm) -> p tm pp t", tm=4)
-            nc.vector.tensor_copy(out=grp[:, 0:2], in_=src[:, 0:2])
-            nc.scalar.copy(out=grp[:, 2:4], in_=src[:, 2:4])
-            return quantise(grp[:].rearrange("p a b c -> p (a b c)"), D, name)
+            nc.scalar.copy(out=grp[:, 3:4], in_=src[:, 3:4])
+            nc.vector.tensor_copy(out=grp[:, 0:3], in_=src[:, 0:3])
+            return grp
 
-        gc_c, gc_s = stationary(gc_raw, "gc")
+        trs, g1s, c1s, pps, a32s, g2s, c2s, pes, negs, exps = {}, {}, {}, {}, {}, {}, {}, {}, {}, {}
+        wts = {}
+
+        def live(T):
+            return 0 <= T < N_TILES
+
+        def st_transpose(T):
+            c, half = divmod(T, 2)
+            raw = raw_chunks[c]
+            trs[T] = []
+            for pair in range(2):
+                tr = ps_tr.tile([P, 2, 2, P], F32, name="tr", tag="tr")
+                for k in range(2):
+                    rw = raw[:, 4 * half + 2 * pair + k, :].bitcast(F32)
+                    for u in range(2):
+                        nc.tensor.transpose(tr[:, k, u, :], rw[:, P * u : P * u + P], ident[:])
+                trs[T].append(tr)
+            if half == 1 and c + 4 < N_TILES // 2:
+                load_chunk(c + 4)
+
+        def st_evac(T):
+            g1 = work.tile([P, 4 * D], BF16, name="g1", tag="g1", align_bytes=64)
+            g1w = g1[:].bitcast(F32).rearrange("p (c jh i u) -> p c jh i u", c=CHUNKS, jh=2, u=2)
+            for pair in range(2):
+                for k in range(2):
+                    nc.scalar.copy(
+                        out=g1w[:, 2 * pair + k],
+                        in_=trs[T][pair][:, k].rearrange("p u (i jh) -> p jh i u", jh=2),
+                    )
+            g1s[T] = g1
+
+        def st_q1(T):
+            c1 = work.tile([P, D], U32, name="c1", tag="c1", align_bytes=64)
+            s1 = work.tile([P, D], U8, name="s1", tag="s1", align_bytes=64)
+            nc.vector.quantize_mx(out=c1[:].bitcast(FP8X4), scales=s1[:], in_=g1s[T][:])
+            c1s[T] = (c1, s1)
+
+        def st_mx(T, ci):
+            b = T // TILES_PER_B
+            c1, s1 = c1s[T]
+            gc_c, gc_s = wts["gc"]
+            ga_c, ga_s = wts["ga"]
+            xr_c, xr_s = wts["xr"]
+            pp = ps_p.tile([P, 4, P], F32, name="pp", tag="pp")
+            for tm in range(4):
+                nc.tensor.matmul_mx(
+                    out=pp[:, tm, :],
+                    lhsT=gc_c[:, P * tm : P * tm + P].bitcast(FP8X4),
+                    lhsT_scale=gc_s[:, P * tm : P * tm + P],
+                    rhs=c1[:, P * ci : P * ci + P].bitcast(FP8X4),
+                    rhs_scale=s1[:, P * ci : P * ci + P],
+                    start=True,
+                    stop=False,
+                )
+                nc.tensor.matmul_mx(
+                    out=pp[:, tm, :],
+                    lhsT=ga_c[:, P * tm : P * tm + P].bitcast(FP8X4),
+                    lhsT_scale=ga_s[:, P * tm : P * tm + P],
+                    rhs=xr_c[:, P * b : P * b + P].bitcast(FP8X4),
+                    rhs_scale=xr_s[:, P * b : P * b + P],
+                    start=False,
+                    stop=True,
+                )
+            pps[(T, ci)] = pp
+
+        def st_add(T, ci):
+            b, g = divmod(T, TILES_PER_B)
+            if ci == 0:
+                a32s[T] = work.tile([P, 4 * D], F32, name="a32", tag="a32")
+            nc.vector.tensor_tensor(
+                out=a32s[T][:, D * ci : D * ci + D].rearrange("p (jh i t) -> p jh i t", jh=2, t=4),
+                in0=pps[(T, ci)][:].rearrange("p t (jh i) -> p jh i t", jh=2),
+                in1=wts["bb"][:, b, :, CHUNKS * g + ci, :].unsqueeze(2).to_broadcast([P, 2, N, 4]),
+                op=ALU.add,
+            )
+
+        def st_tanh(T):
+            g2 = work.tile([P, 4 * D], BF16, name="g2", tag="g2", align_bytes=64)
+            w = 4 * D // TANH_SPLIT
+            for s in range(TANH_SPLIT):
+                nc.scalar.activation(
+                    out=g2[:, w * s : w * s + w], in_=a32s[T][:, w * s : w * s + w], func=ACTF.Tanh
+                )
+            g2s[T] = g2
+
+        def st_q2(T):
+            c2 = work.tile([P, D], U32, name="c2", tag="c2", align_bytes=64)
+            s2 = work.tile([P, D], U8, name="s2", tag="s2", align_bytes=64)
+            nc.vector.quantize_mx(out=c2[:].bitcast(FP8X4), scales=s2[:], in_=g2s[T][:])
+            c2s[T] = (c2, s2)
+
+        def st_e(T):
+            c2, s2 = c2s[T]
+            we_c, we_s = wts["we"]
+            pe = ps_e.tile([P, D], F32, name="pe", tag="pe")
+            nc.tensor.matmul_mx(
+                out=pe[:],
+                lhsT=we_c[:].bitcast(FP8X4),
+                lhsT_scale=we_s[:],
+                rhs=c2[:].bitcast(FP8X4),
+                rhs_scale=s2[:],
+                start=True,
+                stop=True,
+            )
+            pes[T] = pe
+
+        def st_negmax(T):
+            negmax = small.tile([P, 8], F32, name="negmax", tag="negmax")
+            nc.vector.tensor_reduce(
+                out=negmax[:],
+                in_=pes[T][:].rearrange("p (j i) -> p j i", j=8),
+                axis=AX.X,
+                op=ALU.max,
+                negate=True,
+            )
+            negs[T] = negmax
+
+        def st_exp(T):
+            pexp = work.tile([P, D], F32, name="pexp", tag="pexp")
+            ssum = small.tile([P, 8], F32, name="ssum", tag="ssum")
+            for j in range(8):
+                nc.scalar.activation(
+                    out=pexp[:, N * j : N * j + N],
+                    in_=pes[T][:, N * j : N * j + N],
+                    func=ACTF.Exp,
+                    bias=negs[T][:, j : j + 1],
+                    scale=1.0,
+                    accum_out=ssum[:, j : j + 1],
+                )
+            exps[T] = (pexp, ssum)
+
+        acc8 = const.tile([P, B, 8, N], F32, name="acc8")
+        osum = const.tile([P, B * N], F32, name="osum")
+        besa = const.tile([P, 1], F32, name="besa")
+
+        def st_weigh(T):
+            b, g = divmod(T, TILES_PER_B)
+            pexp, ssum = exps[T]
+            rinv = small.tile([P, 8], F32, name="rinv", tag="rinv")
+            nc.vector.reciprocal(out=rinv[:], in_=ssum[:])
+            q = work.tile([P, 8, N], F32, name="q", tag="q")
+            nc.vector.scalar_tensor_tensor(
+                out=q[:].rearrange("p j i -> p (j i)"),
+                in0=pes[T][:],
+                scalar=besa[:, 0:1],
+                in1=pexp[:],
+                op0=ALU.add,
+                op1=ALU.mult,
+            )
+            if T < GPS_TILES:
+                r_b = rinv[:].unsqueeze(2).to_broadcast([P, 8, N])
+                if g == 0:
+                    nc.gpsimd.tensor_tensor(out=acc8[:, b], in0=q[:], in1=r_b, op=ALU.mult)
+                else:
+                    wq = work.tile([P, 8, N], F32, name="wq", tag="wq")
+                    nc.gpsimd.tensor_tensor(out=wq[:], in0=q[:], in1=r_b, op=ALU.mult)
+                    nc.gpsimd.tensor_tensor(out=acc8[:, b], in0=acc8[:, b], in1=wq[:], op=ALU.add)
+            else:
+                for j in range(8):
+                    nc.vector.scalar_tensor_tensor(
+                        out=acc8[:, b, j, :],
+                        in0=q[:, j, :],
+                        scalar=rinv[:, j : j + 1],
+                        in1=acc8[:, b, j, :],
+                        op0=ALU.mult,
+                        op1=ALU.add,
+                    )
+
+        def sum_partials(b):
+            nc.vector.tensor_reduce(
+                out=osum[:, N * b : N * b + N],
+                in_=acc8[:, b].rearrange("p j i -> p i j"),
+                axis=AX.X,
+                op=ALU.add,
+            )
+
+        def store_pair(h):
+            pf = ps_tr.tile([P, 2, 2, P], F32, name="pf", tag="tr")
+            nc.tensor.transpose(pf[:, 0, 0, :], osum[:, P * h : P * h + P], ident[:])
+            ot = work.tile([P, P], F32, name="ot", tag="ot")
+            nc.vector.tensor_copy(out=ot[:], in_=pf[:, 0, 0, :])
+            nc.sync.dma_start(
+                out=out_1.rearrange("b i c -> (b i) c")[P * h : P * h + P, :], in_=ot[:]
+            )
 
         x_tr = ps_tr.tile([P, 2, 2, P], F32, name="x_tr", tag="tr")
         for r in range(2):
@@ -112,20 +301,24 @@ def tile_languagemsgencoder_pb_t_kernel(
             out=xrep[:].bitcast(F32).rearrange("p (b r w) -> p b r w", b=B, r=2),
             in_=xgw.rearrange("p (b w) -> p b w", b=B).unsqueeze(2).to_broadcast([P, B, 2, 2 * N]),
         )
-        x_c, x_s = quantise(xg[:], B * N, "x")
-        xr_c, xr_s = quantise(xrep[:], B * 2 * N, "xr")
-
-        ga_c, ga_s = stationary(ga_raw, "ga")
-        gb_c, gb_s = stationary(gb_raw, "gb")
+        st_transpose(0)
+        wts["x"] = quantise(xg[:], B * N, "x")
+        gb_grp = regroup_stationary(gb_raw)
+        wts["xr"] = quantise(xrep[:], B * 2 * N, "xr")
+        gc_grp = regroup_stationary(gc_raw)
+        wts["gb"] = quantise(gb_grp[:].rearrange("p a b c -> p (a b c)"), D, "gb")
+        st_evac(0)
+        st_transpose(1)
 
         bgr = const.tile([P, 4], F32, name="bgr")
         nc.vector.tensor_copy(out=bgr[:], in_=bgr_bf[:])
-        besa = const.tile([P, 1], F32, name="besa")
         nc.vector.tensor_copy(out=besa[:], in_=besa_bf[:])
-
         bb = const.tile([P, B * N, 4], F32, name="bb")
+        x_c, x_s = wts["x"]
+        gb_c, gb_s = wts["gb"]
+        pbs = []
         for h in range(2):
-            pb = ps_p.tile([P, 4, P], F32, name="pb", tag="pp")
+            pb = ps_e.tile([P, 4, P], F32, name="pb", tag="pe")
             for tm in range(4):
                 nc.tensor.matmul_mx(
                     out=pb[:, tm, :],
@@ -136,177 +329,95 @@ def tile_languagemsgencoder_pb_t_kernel(
                     start=True,
                     stop=True,
                 )
+            pbs.append(pb)
+        ga_grp = regroup_stationary(ga_raw)
+        wts["gc"] = quantise(gc_grp[:].rearrange("p a b c -> p (a b c)"), D, "gc")
+        for h in range(2):
             nc.vector.tensor_tensor(
                 out=bb[:, P * h : P * h + P, :],
-                in0=pb[:].rearrange("p t c -> p c t"),
+                in0=pbs[h][:].rearrange("p t c -> p c t"),
                 in1=bgr[:].unsqueeze(1).to_broadcast([P, P, 4]),
                 op=ALU.add,
             )
-        bb_v = bb[:].rearrange("p (b jh n) t -> p b jh n t", b=B, jh=2)
+        wts["bb"] = bb[:].rearrange("p (b jh n) t -> p b jh n t", b=B, jh=2)
+        wts["ga"] = quantise(ga_grp[:].rearrange("p a b c -> p (a b c)"), D, "ga")
 
-        we_grp = const.tile([P, F, 4], BF16, name="we_grp", align_bytes=64)
-        nc.vector.tensor_copy(out=we_grp[:], in_=we_raw[:].rearrange("p t n -> p n t"))
-        we_c, we_s = quantise(we_grp[:].rearrange("p n t -> p (n t)"), F, "we")
+        def prepare_w_esa():
+            we_grp = const.tile([P, F, 4], BF16, name="we_grp", align_bytes=64)
+            nc.vector.tensor_copy(out=we_grp[:], in_=we_raw[:].rearrange("p t n -> p n t"))
+            wts["we"] = quantise(we_grp[:].rearrange("p n t -> p (n t)"), F, "we")
 
-        acc8 = const.tile([P, B, 8, N], F32, name="acc8")
-        osum = const.tile([P, B * N], F32, name="osum")
+        nxs = {}
 
-        def new_x():
-            go_grp = wtmp.tile([P, D, 4], BF16, name="go_grp", tag="grp", align_bytes=64)
+        def nx_weights():
+            go_grp = wtmp.tile([P, D, 4], BF16, name="go_grp", tag="grp", bufs=3, align_bytes=64)
             nc.vector.tensor_copy(out=go_grp[:], in_=go_raw[:].rearrange("p t c -> p c t"))
-            go_c, go_s = quantise(go_grp[:].rearrange("p c t -> p (c t)"), D, "go")
-            out_rows = out_0.rearrange("b n d -> (b n) d")
-            for r in range(2):
-                px = ps_e.tile([P, D], F32, name="px", tag="pe")
-                nc.tensor.matmul_mx(
-                    out=px[:],
-                    lhsT=x_c[:, P * r : P * r + P].bitcast(FP8X4),
-                    lhsT_scale=x_s[:, P * r : P * r + P],
-                    rhs=go_c[:].bitcast(FP8X4),
-                    rhs_scale=go_s[:],
-                    start=True,
-                    stop=True,
-                )
-                nx = work.tile([P, D], F32, name="nx", tag="pq")
-                nc.vector.tensor_tensor(out=nx[:], in0=px[:], in1=bgo_bc[:], op=ALU.add)
-                nxt = work.tile([P, D], F32, name="nxt", tag="pq")
-                nc.scalar.activation(out=nxt[:], in_=nx[:], func=ACTF.Tanh)
-                nc.sync.dma_start(out=out_rows[P * r : P * r + P, :], in_=nxt[:])
+            wts["go"] = quantise(go_grp[:].rearrange("p c t -> p (c t)"), D, "go")
 
-        def finish_pair(h):
-            for b in (2 * h, 2 * h + 1):
-                nc.vector.tensor_reduce(
-                    out=osum[:, N * b : N * b + N],
-                    in_=acc8[:, b].rearrange("p j i -> p i j"),
-                    axis=AX.X,
-                    op=ALU.add,
-                )
-            pf = ps_e.tile([P, D], F32, name="pf", tag="pe")
-            nc.tensor.transpose(pf[:, 0:P], osum[:, P * h : P * h + P], ident[:])
-            ot = work.tile([P, P], F32, name="ot", tag="ot")
-            nc.vector.tensor_copy(out=ot[:], in_=pf[:, 0:P])
-            nc.sync.dma_start(
-                out=out_1.rearrange("b i c -> (b i) c")[P * h : P * h + P, :], in_=ot[:]
-            )
-
-        n_tiles = B * TILES_PER_B
-        for T in range(n_tiles):
-            b, g = divmod(T, TILES_PER_B)
-            c, half = divmod(T, 2)
-            if half == 0 and c + 2 < n_tiles // 2:
-                load_chunk(c + 2)
-            raw = raw_chunks[c]
-
-            g1 = work.tile([P, 4 * D], BF16, name="g1", tag="g1", align_bytes=64)
-            g1w = g1[:].bitcast(F32).rearrange("p (c jh i u) -> p c jh i u", c=CHUNKS, jh=2, u=2)
-            for pair in range(2):
-                tr = ps_tr.tile([P, 2, 2, P], F32, name="tr", tag="tr")
-                for k in range(2):
-                    rw = raw[:, 4 * half + 2 * pair + k, :].bitcast(F32)
-                    for u in range(2):
-                        nc.tensor.transpose(tr[:, k, u, :], rw[:, P * u : P * u + P], ident[:])
-                for k in range(2):
-                    nc.scalar.copy(
-                        out=g1w[:, 2 * pair + k],
-                        in_=tr[:, k].rearrange("p u (i jh) -> p jh i u", jh=2),
-                    )
-            c1 = work.tile([P, D], U32, name="c1", tag="c1", align_bytes=64)
-            s1 = work.tile([P, D], U8, name="s1", tag="s1", align_bytes=64)
-            nc.vector.quantize_mx(out=c1[:].bitcast(FP8X4), scales=s1[:], in_=g1[:])
-
-            a32 = work.tile([P, 4 * D], F32, name="a32", tag="a32")
-            for ci in range(CHUNKS):
-                n = CHUNKS * g + ci
-                pp = ps_p.tile([P, 4, P], F32, name="pp", tag="pp")
-                for tm in range(4):
-                    nc.tensor.matmul_mx(
-                        out=pp[:, tm, :],
-                        lhsT=gc_c[:, P * tm : P * tm + P].bitcast(FP8X4),
-                        lhsT_scale=gc_s[:, P * tm : P * tm + P],
-                        rhs=c1[:, P * ci : P * ci + P].bitcast(FP8X4),
-                        rhs_scale=s1[:, P * ci : P * ci + P],
-                        start=True,
-                        stop=False,
-                    )
-                    nc.tensor.matmul_mx(
-                        out=pp[:, tm, :],
-                        lhsT=ga_c[:, P * tm : P * tm + P].bitcast(FP8X4),
-                        lhsT_scale=ga_s[:, P * tm : P * tm + P],
-                        rhs=xr_c[:, P * b : P * b + P].bitcast(FP8X4),
-                        rhs_scale=xr_s[:, P * b : P * b + P],
-                        start=False,
-                        stop=True,
-                    )
-                nc.vector.tensor_tensor(
-                    out=a32[:, D * ci : D * ci + D].rearrange("p (jh i t) -> p jh i t", jh=2, t=4),
-                    in0=pp[:].rearrange("p t (jh i) -> p jh i t", jh=2),
-                    in1=bb_v[:, b, :, n, :].unsqueeze(2).to_broadcast([P, 2, N, 4]),
-                    op=ALU.add,
-                )
-            g2 = work.tile([P, 4 * D], BF16, name="g2", tag="g2", align_bytes=64)
-            w = 4 * D // TANH_SPLIT
-            for s in range(TANH_SPLIT):
-                nc.scalar.activation(
-                    out=g2[:, w * s : w * s + w], in_=a32[:, w * s : w * s + w], func=ACTF.Tanh
-                )
-            c2 = work.tile([P, D], U32, name="c2", tag="c2", align_bytes=64)
-            s2 = work.tile([P, D], U8, name="s2", tag="s2", align_bytes=64)
-            nc.vector.quantize_mx(out=c2[:].bitcast(FP8X4), scales=s2[:], in_=g2[:])
-
-            pe = ps_e.tile([P, D], F32, name="pe", tag="pe")
+        def nx_matmul(r):
+            go_c, go_s = wts["go"]
+            px = ps_p.tile([P, D], F32, name="px", tag="pp")
             nc.tensor.matmul_mx(
-                out=pe[:],
-                lhsT=we_c[:].bitcast(FP8X4),
-                lhsT_scale=we_s[:],
-                rhs=c2[:].bitcast(FP8X4),
-                rhs_scale=s2[:],
+                out=px[:],
+                lhsT=x_c[:, P * r : P * r + P].bitcast(FP8X4),
+                lhsT_scale=x_s[:, P * r : P * r + P],
+                rhs=go_c[:].bitcast(FP8X4),
+                rhs_scale=go_s[:],
                 start=True,
                 stop=True,
             )
-            negmax = small.tile([P, 8], F32, name="negmax", tag="negmax")
-            nc.vector.tensor_reduce(
-                out=negmax[:],
-                in_=pe[:].rearrange("p (j i) -> p j i", j=8),
-                axis=AX.X,
-                op=ALU.max,
-                negate=True,
+            nxs[r] = px
+
+        def nx_add(r):
+            nx = work.tile([P, D], F32, name="nx", tag="nx", bufs=2)
+            nc.vector.tensor_tensor(out=nx[:], in0=nxs[r][:], in1=bgo_bc[:], op=ALU.add)
+            nxs[r] = nx
+
+        def nx_tanh(r):
+            nxt = work.tile([P, D], F32, name="nxt", tag="nxt", bufs=2)
+            nc.scalar.activation(out=nxt[:], in_=nxs[r][:], func=ACTF.Tanh)
+            nc.sync.dma_start(
+                out=out_0.rearrange("b n d -> (b n) d")[P * r : P * r + P, :], in_=nxt[:]
             )
-            pexp = work.tile([P, D], F32, name="pexp", tag="pexp")
-            ssum = small.tile([P, 8], F32, name="ssum", tag="ssum")
-            for j in range(8):
-                nc.scalar.activation(
-                    out=pexp[:, N * j : N * j + N],
-                    in_=pe[:, N * j : N * j + N],
-                    func=ACTF.Exp,
-                    bias=negmax[:, j : j + 1],
-                    scale=1.0,
-                    accum_out=ssum[:, j : j + 1],
-                )
-            rinv = small.tile([P, 8], F32, name="rinv", tag="rinv")
-            nc.vector.reciprocal(out=rinv[:], in_=ssum[:])
-            q = work.tile([P, D], F32, name="q", tag="pq")
-            nc.vector.scalar_tensor_tensor(
-                out=q[:], in0=pe[:], scalar=besa[:, 0:1], in1=pexp[:], op0=ALU.add, op1=ALU.mult
-            )
-            for j in range(8):
-                if g == 0:
-                    nc.vector.tensor_scalar(
-                        out=acc8[:, b, j, :],
-                        in0=q[:, N * j : N * j + N],
-                        scalar1=rinv[:, j : j + 1],
-                        scalar2=None,
-                        op0=ALU.mult,
-                    )
-                else:
-                    nc.vector.scalar_tensor_tensor(
-                        out=acc8[:, b, j, :],
-                        in0=q[:, N * j : N * j + N],
-                        scalar=rinv[:, j : j + 1],
-                        in1=acc8[:, b, j, :],
-                        op0=ALU.mult,
-                        op1=ALU.add,
-                    )
+
+        for T in range(-1, N_TILES + 4):
+            if live(T - 2):
+                st_q2(T - 2)
+                st_e(T - 2)
+            if live(T + 1):
+                st_q1(T + 1)
+            if live(T - 3):
+                st_exp(T - 3)
+                st_weigh(T - 3)
+            if T == N_TILES + 1:
+                nx_add(0)
+            for ci in range(CHUNKS):
+                if live(T):
+                    st_add(T, ci)
+                if live(T + 1):
+                    st_mx(T + 1, ci)
+            if live(T + 2):
+                st_evac(T + 2)
+            if live(T + 3):
+                st_transpose(T + 3)
             if T == 1:
-                new_x()
-            if g == TILES_PER_B - 1 and b % 2 == 1:
-                finish_pair(b // 2)
+                prepare_w_esa()
+            if live(T - 1):
+                st_tanh(T - 1)
+            if live(T - 2):
+                st_negmax(T - 2)
+            if T == N_TILES:
+                nx_weights()
+                nx_matmul(0)
+                nx_matmul(1)
+                sum_partials(0)
+                sum_partials(1)
+                store_pair(0)
+            if T == N_TILES + 1:
+                nx_tanh(0)
+                nx_add(1)
+                sum_partials(2)
+            if T == N_TILES + 2:
+                nx_tanh(1)
+        sum_partials(3)
+        store_pair(1)

@@ -20,7 +20,7 @@ TILES_PER_B = 8
 N_TILES = B * TILES_PER_B
 CHUNKS = 4
 TANH_SPLIT = 2
-GPS_TILES = N_TILES - 1
+GPS_TILES = N_TILES - 3
 
 
 def tile_languagemsgencoder_pb_t_kernel(
@@ -81,9 +81,9 @@ def tile_languagemsgencoder_pb_t_kernel(
         ga_raw = load_k_first(W_gr[0:D, :], "ga_raw")
         load_chunk(1)
         nc.sync.dma_start(out=we_raw[:], in_=W_esa.rearrange("(p t) n -> p t n", t=4))
+        go_raw = load_k_first(W_go, "go_raw")
         load_chunk(2)
         load_chunk(3)
-        go_raw = load_k_first(W_go, "go_raw")
         bgo_bc = const.tile([P, D], BF16, name="bgo_bc")
         nc.sync.dma_start(out=bgo_bc[:], in_=b_go.partition_broadcast(P))
 
@@ -235,11 +235,11 @@ def tile_languagemsgencoder_pb_t_kernel(
         osum = const.tile([P, B * N], F32, name="osum")
         besa = const.tile([P, 1], F32, name="besa")
 
-        def st_weigh(T):
-            b, g = divmod(T, TILES_PER_B)
+        qs, rinvs = {}, {}
+
+        def st_q(T):
+            b = T // TILES_PER_B
             pexp, ssum = exps[T]
-            rinv = small.tile([P, 8], F32, name="rinv", tag="rinv")
-            nc.vector.reciprocal(out=rinv[:], in_=ssum[:])
             q = work.tile([P, 8, N], F32, name="q", tag="q")
             nc.vector.scalar_tensor_tensor(
                 out=q[:].rearrange("p j i -> p (j i)"),
@@ -249,15 +249,10 @@ def tile_languagemsgencoder_pb_t_kernel(
                 op0=ALU.add,
                 op1=ALU.mult,
             )
-            if T < GPS_TILES:
-                r_b = rinv[:].unsqueeze(2).to_broadcast([P, 8, N])
-                if g == 0:
-                    nc.gpsimd.tensor_tensor(out=acc8[:, b], in0=q[:], in1=r_b, op=ALU.mult)
-                else:
-                    wq = work.tile([P, 8, N], F32, name="wq", tag="wq")
-                    nc.gpsimd.tensor_tensor(out=wq[:], in0=q[:], in1=r_b, op=ALU.mult)
-                    nc.gpsimd.tensor_tensor(out=acc8[:, b], in0=acc8[:, b], in1=wq[:], op=ALU.add)
-            else:
+            qs[T] = q
+            if T >= GPS_TILES:
+                rinv = small.tile([P, 8], F32, name="rinv", tag="rinv")
+                nc.vector.reciprocal(out=rinv[:], in_=ssum[:])
                 for j in range(8):
                     nc.vector.scalar_tensor_tensor(
                         out=acc8[:, b, j, :],
@@ -267,6 +262,24 @@ def tile_languagemsgencoder_pb_t_kernel(
                         op0=ALU.mult,
                         op1=ALU.add,
                     )
+
+        def st_gps(T, half):
+            b, g = divmod(T, TILES_PER_B)
+            if half == 0:
+                rinvs[T] = small.tile([P, 8], F32, name="rinv", tag="rinv")
+            rinv = rinvs[T]
+            js = slice(4 * half, 4 * half + 4)
+            nc.vector.reciprocal(out=rinv[:, js], in_=exps[T][1][:, js])
+            r_b = rinv[:, js].unsqueeze(2).to_broadcast([P, 4, N])
+            q = qs[T]
+            if g == 0:
+                nc.gpsimd.tensor_tensor(out=acc8[:, b, js, :], in0=q[:, js, :], in1=r_b, op=ALU.mult)
+            else:
+                wq = work.tile([P, 4, N], F32, name="wq", tag="wq")
+                nc.gpsimd.tensor_tensor(out=wq[:], in0=q[:, js, :], in1=r_b, op=ALU.mult)
+                nc.gpsimd.tensor_tensor(
+                    out=acc8[:, b, js, :], in0=acc8[:, b, js, :], in1=wq[:], op=ALU.add
+                )
 
         def sum_partials(b):
             nc.vector.tensor_reduce(
@@ -301,12 +314,12 @@ def tile_languagemsgencoder_pb_t_kernel(
             out=xrep[:].bitcast(F32).rearrange("p (b r w) -> p b r w", b=B, r=2),
             in_=xgw.rearrange("p (b w) -> p b w", b=B).unsqueeze(2).to_broadcast([P, B, 2, 2 * N]),
         )
-        st_transpose(0)
         wts["x"] = quantise(xg[:], B * N, "x")
         gb_grp = regroup_stationary(gb_raw)
         wts["xr"] = quantise(xrep[:], B * 2 * N, "xr")
         gc_grp = regroup_stationary(gc_raw)
         wts["gb"] = quantise(gb_grp[:].rearrange("p a b c -> p (a b c)"), D, "gb")
+        st_transpose(0)
         st_evac(0)
         st_transpose(1)
 
@@ -349,9 +362,12 @@ def tile_languagemsgencoder_pb_t_kernel(
 
         nxs = {}
 
-        def nx_weights():
-            go_grp = wtmp.tile([P, D, 4], BF16, name="go_grp", tag="grp", bufs=3, align_bytes=64)
-            nc.vector.tensor_copy(out=go_grp[:], in_=go_raw[:].rearrange("p t c -> p c t"))
+        go_grp = const.tile([P, D, 4], BF16, name="go_grp", align_bytes=64)
+
+        def nx_regroup():
+            nc.scalar.copy(out=go_grp[:], in_=go_raw[:].rearrange("p t c -> p c t"))
+
+        def nx_quantise():
             wts["go"] = quantise(go_grp[:].rearrange("p c t -> p (c t)"), D, "go")
 
         def nx_matmul(r):
@@ -380,44 +396,71 @@ def tile_languagemsgencoder_pb_t_kernel(
                 out=out_0.rearrange("b n d -> (b n) d")[P * r : P * r + P, :], in_=nxt[:]
             )
 
-        for T in range(-1, N_TILES + 4):
+        def gps(T, half):
+            if 0 <= T < GPS_TILES:
+                st_gps(T, half)
+
+        def add_then_mx(T, ci):
+            if live(T):
+                st_add(T, ci)
+            if live(T + 1):
+                st_mx(T + 1, ci)
+
+        for T in range(-2, N_TILES):
             if live(T - 2):
                 st_q2(T - 2)
                 st_e(T - 2)
-            if live(T + 1):
-                st_q1(T + 1)
             if live(T - 3):
                 st_exp(T - 3)
-                st_weigh(T - 3)
-            if T == N_TILES + 1:
-                nx_add(0)
-            for ci in range(CHUNKS):
-                if live(T):
-                    st_add(T, ci)
-                if live(T + 1):
-                    st_mx(T + 1, ci)
+            gps(T - 4, 0)
+            add_then_mx(T, 0)
+            if live(T - 3):
+                st_q(T - 3)
+            add_then_mx(T, 1)
             if live(T + 2):
-                st_evac(T + 2)
-            if live(T + 3):
-                st_transpose(T + 3)
+                st_q1(T + 2)
+            gps(T - 4, 1)
+            add_then_mx(T, 2)
             if T == 1:
                 prepare_w_esa()
             if live(T - 1):
                 st_tanh(T - 1)
             if live(T - 2):
                 st_negmax(T - 2)
-            if T == N_TILES:
-                nx_weights()
-                nx_matmul(0)
-                nx_matmul(1)
-                sum_partials(0)
-                sum_partials(1)
-                store_pair(0)
-            if T == N_TILES + 1:
-                nx_tanh(0)
-                nx_add(1)
-                sum_partials(2)
-            if T == N_TILES + 2:
-                nx_tanh(1)
+            add_then_mx(T, 3)
+            if live(T + 3):
+                st_evac(T + 3)
+            if T == 0:
+                nx_regroup()
+            if live(T + 4):
+                st_transpose(T + 4)
+
+        L = N_TILES - 1
+        st_q2(L - 1)
+        st_e(L - 1)
+        st_exp(L - 2)
+        gps(L - 3, 0)
+        st_q(L - 2)
+        gps(L - 3, 1)
+        st_tanh(L)
+        nx_quantise()
+        nx_matmul(0)
+        nx_matmul(1)
+        st_negmax(L - 1)
+        sum_partials(0)
+        st_q2(L)
+        st_e(L)
+        st_exp(L - 1)
+        nx_add(0)
+        nx_tanh(0)
+        st_negmax(L)
+        st_exp(L)
+        nx_add(1)
+        nx_tanh(1)
+        st_q(L - 1)
+        sum_partials(1)
+        store_pair(0)
+        sum_partials(2)
+        st_q(L)
         sum_partials(3)
         store_pair(1)

@@ -19,7 +19,6 @@ FLOPS = 2 * (3 * B * N * D * D + B * N * N * D * D + B * N * N * D * F)
 TILES_PER_B = 8
 N_TILES = B * TILES_PER_B
 CHUNKS = 4
-TANH_SPLIT = 2
 GPS_TILES = N_TILES - 3
 
 
@@ -143,23 +142,25 @@ def tile_languagemsgencoder_pb_t_kernel(
             gc_c, gc_s = wts["gc"]
             ga_c, ga_s = wts["ga"]
             xr_c, xr_s = wts["xr"]
-            pp = ps_p.tile([P, 4, P], F32, name="pp", tag="pp")
-            for tm in range(4):
+            h, tp = divmod(ci, 2)
+            pp = ps_p.tile([P, 2, 2 * P], F32, name="pp", tag="pp")
+            for e in range(2):
+                tm = 2 * tp + e
                 nc.tensor.matmul_mx(
-                    out=pp[:, tm, :],
+                    out=pp[:, e, :],
                     lhsT=gc_c[:, P * tm : P * tm + P].bitcast(FP8X4),
                     lhsT_scale=gc_s[:, P * tm : P * tm + P],
-                    rhs=c1[:, P * ci : P * ci + P].bitcast(FP8X4),
-                    rhs_scale=s1[:, P * ci : P * ci + P],
+                    rhs=c1[:, 2 * P * h : 2 * P * h + 2 * P].bitcast(FP8X4),
+                    rhs_scale=s1[:, 2 * P * h : 2 * P * h + 2 * P],
                     start=True,
                     stop=False,
                 )
                 nc.tensor.matmul_mx(
-                    out=pp[:, tm, :],
+                    out=pp[:, e, :],
                     lhsT=ga_c[:, P * tm : P * tm + P].bitcast(FP8X4),
                     lhsT_scale=ga_s[:, P * tm : P * tm + P],
-                    rhs=xr_c[:, P * b : P * b + P].bitcast(FP8X4),
-                    rhs_scale=xr_s[:, P * b : P * b + P],
+                    rhs=xr_c[:, 2 * P * b : 2 * P * b + 2 * P].bitcast(FP8X4),
+                    rhs_scale=xr_s[:, 2 * P * b : 2 * P * b + 2 * P],
                     start=False,
                     stop=True,
                 )
@@ -167,21 +168,27 @@ def tile_languagemsgencoder_pb_t_kernel(
 
         def st_add(T, ci):
             b, g = divmod(T, TILES_PER_B)
+            h, tp = divmod(ci, 2)
             if ci == 0:
-                a32s[T] = work.tile([P, 4 * D], F32, name="a32", tag="a32")
+                a32s[T] = work.tile([P, 2, 2, 2 * P, 2], F32, name="a32", tag="a32")
+            first = 2 * (CHUNKS * g + 2 * h)
             nc.vector.tensor_tensor(
-                out=a32s[T][:, D * ci : D * ci + D].rearrange("p (jh i t) -> p jh i t", jh=2, t=4),
-                in0=pps[(T, ci)][:].rearrange("p t (jh i) -> p jh i t", jh=2),
-                in1=wts["bb"][:, b, :, CHUNKS * g + ci, :].unsqueeze(2).to_broadcast([P, 2, N, 4]),
+                out=a32s[T][:, h, tp].rearrange("p (g i) e -> p g i e", g=4),
+                in0=pps[(T, ci)][:].rearrange("p e (g i) -> p g i e", g=4),
+                in1=wts["bb"][:, b, first : first + 4, 2 * tp : 2 * tp + 2]
+                .unsqueeze(2)
+                .to_broadcast([P, 4, N, 2]),
                 op=ALU.add,
             )
 
         def st_tanh(T):
             g2 = work.tile([P, 4 * D], BF16, name="g2", tag="g2", align_bytes=64)
-            w = 4 * D // TANH_SPLIT
-            for s in range(TANH_SPLIT):
+            w = 4 * D // 2
+            for h in range(2):
                 nc.scalar.activation(
-                    out=g2[:, w * s : w * s + w], in_=a32s[T][:, w * s : w * s + w], func=ACTF.Tanh
+                    out=g2[:, w * h : w * h + w].rearrange("p (w tp e) -> p w tp e", tp=2, e=2),
+                    in_=a32s[T][:, h].rearrange("p tp w e -> p w tp e"),
+                    func=ACTF.Tanh,
                 )
             g2s[T] = g2
 
@@ -309,14 +316,14 @@ def tile_languagemsgencoder_pb_t_kernel(
             out=xgw.rearrange("p (r c u) -> p r c u", r=2, u=2),
             in_=x_tr[:].rearrange("p r u c -> p r c u"),
         )
-        xrep = const.tile([P, 4 * B * 2 * N], BF16, name="xrep", align_bytes=64)
+        xrep = const.tile([P, 4 * B * 4 * N], BF16, name="xrep", align_bytes=64)
         nc.vector.tensor_copy(
-            out=xrep[:].bitcast(F32).rearrange("p (b r w) -> p b r w", b=B, r=2),
-            in_=xgw.rearrange("p (b w) -> p b w", b=B).unsqueeze(2).to_broadcast([P, B, 2, 2 * N]),
+            out=xrep[:].bitcast(F32).rearrange("p (b r w) -> p b r w", b=B, r=4),
+            in_=xgw.rearrange("p (b w) -> p b w", b=B).unsqueeze(2).to_broadcast([P, B, 4, 2 * N]),
         )
         wts["x"] = quantise(xg[:], B * N, "x")
         gb_grp = regroup_stationary(gb_raw)
-        wts["xr"] = quantise(xrep[:], B * 2 * N, "xr")
+        wts["xr"] = quantise(xrep[:], B * 4 * N, "xr")
         gc_grp = regroup_stationary(gc_raw)
         wts["gb"] = quantise(gb_grp[:].rearrange("p a b c -> p (a b c)"), D, "gb")
         st_transpose(0)
@@ -326,7 +333,7 @@ def tile_languagemsgencoder_pb_t_kernel(
         bgr = const.tile([P, 4], F32, name="bgr")
         nc.vector.tensor_copy(out=bgr[:], in_=bgr_bf[:])
         nc.vector.tensor_copy(out=besa[:], in_=besa_bf[:])
-        bb = const.tile([P, B * N, 4], F32, name="bb")
+        bb = const.tile([P, B, N // 2, 2, 4], F32, name="bb")
         x_c, x_s = wts["x"]
         gb_c, gb_s = wts["gb"]
         pbs = []
@@ -345,14 +352,15 @@ def tile_languagemsgencoder_pb_t_kernel(
             pbs.append(pb)
         ga_grp = regroup_stationary(ga_raw)
         wts["gc"] = quantise(gc_grp[:].rearrange("p a b c -> p (a b c)"), D, "gc")
-        for h in range(2):
+        for b in range(B):
+            h, bl = divmod(b, 2)
             nc.vector.tensor_tensor(
-                out=bb[:, P * h : P * h + P, :],
-                in0=pbs[h][:].rearrange("p t c -> p c t"),
-                in1=bgr[:].unsqueeze(1).to_broadcast([P, P, 4]),
+                out=bb[:, b].rearrange("p n jh t -> p jh n t"),
+                in0=pbs[h][:, :, N * bl : N * bl + N].rearrange("p t (jh n) -> p jh n t", jh=2),
+                in1=bgr[:].unsqueeze(1).unsqueeze(1).to_broadcast([P, 2, N // 2, 4]),
                 op=ALU.add,
             )
-        wts["bb"] = bb[:].rearrange("p (b jh n) t -> p b jh n t", b=B, jh=2)
+        wts["bb"] = bb[:].rearrange("p b n jh t -> p b (n jh) t")
         wts["ga"] = quantise(ga_grp[:].rearrange("p a b c -> p (a b c)"), D, "ga")
 
         def prepare_w_esa():

@@ -19,6 +19,7 @@ FLOPS = 2 * (3 * B * N * D * D + B * N * N * D * D + B * N * N * D * F)
 TILES_PER_B = 8
 N_TILES = B * TILES_PER_B
 CHUNKS = 4
+VEC_EVAC_EVERY = 2
 GPS_TILES = N_TILES - 3
 
 
@@ -123,6 +124,12 @@ def tile_languagemsgencoder_pb_t_kernel(
             g1 = work.tile([P, 4 * D], BF16, name="g1", tag="g1", align_bytes=64)
             g1w = g1[:].bitcast(F32).rearrange("p (c jh i u) -> p c jh i u", c=CHUNKS, jh=2, u=2)
             for pair in range(2):
+                if pair == 1 and T % VEC_EVAC_EVERY == VEC_EVAC_EVERY - 1:
+                    nc.vector.tensor_copy(
+                        out=g1w[:, 2 * pair : 2 * pair + 2],
+                        in_=trs[T][pair][:].rearrange("p k u (i jh) -> p k jh i u", jh=2),
+                    )
+                    continue
                 for k in range(2):
                     nc.scalar.copy(
                         out=g1w[:, 2 * pair + k],

@@ -7,6 +7,7 @@ F32 = mybir.dt.float32
 BF16 = mybir.dt.bfloat16
 U32 = mybir.dt.uint32
 U8 = mybir.dt.uint8
+I32 = mybir.dt.int32
 FP8X4 = mybir.dt.float8_e4m3fn_x4
 ACTF = mybir.ActivationFunctionType
 ALU = mybir.AluOpType
@@ -19,8 +20,7 @@ FLOPS = 2 * (3 * B * N * D * D + B * N * N * D * D + B * N * N * D * F)
 TILES_PER_B = 8
 N_TILES = B * TILES_PER_B
 CHUNKS = 4
-VEC_EVAC_EVERY = 2
-GPS_TILES = N_TILES - 3
+GPS_TILES = N_TILES - 2
 
 
 def tile_languagemsgencoder_pb_t_kernel(
@@ -96,8 +96,8 @@ def tile_languagemsgencoder_pb_t_kernel(
         def regroup_stationary(raw):
             grp = wtmp.tile([P, 4, P, 4], BF16, name="grp", tag="grp", bufs=3, align_bytes=64)
             src = raw[:].rearrange("p t (pp tm) -> p tm pp t", tm=4)
-            nc.scalar.copy(out=grp[:, 3:4], in_=src[:, 3:4])
-            nc.vector.tensor_copy(out=grp[:, 0:3], in_=src[:, 0:3])
+            nc.scalar.copy(out=grp[:, 2:4], in_=src[:, 2:4])
+            nc.vector.tensor_copy(out=grp[:, 0:2], in_=src[:, 0:2])
             return grp
 
         trs, g1s, c1s, pps, a32s, g2s, c2s, pes, negs, exps = {}, {}, {}, {}, {}, {}, {}, {}, {}, {}
@@ -124,12 +124,6 @@ def tile_languagemsgencoder_pb_t_kernel(
             g1 = work.tile([P, 4 * D], BF16, name="g1", tag="g1", align_bytes=64)
             g1w = g1[:].bitcast(F32).rearrange("p (c jh i u) -> p c jh i u", c=CHUNKS, jh=2, u=2)
             for pair in range(2):
-                if pair == 1 and T % VEC_EVAC_EVERY == VEC_EVAC_EVERY - 1:
-                    nc.vector.tensor_copy(
-                        out=g1w[:, 2 * pair : 2 * pair + 2],
-                        in_=trs[T][pair][:].rearrange("p k u (i jh) -> p k jh i u", jh=2),
-                    )
-                    continue
                 for k in range(2):
                     nc.scalar.copy(
                         out=g1w[:, 2 * pair + k],
@@ -249,24 +243,34 @@ def tile_languagemsgencoder_pb_t_kernel(
         osum = const.tile([P, B * N], F32, name="osum")
         besa = const.tile([P, 1], F32, name="besa")
 
-        qs, rinvs = {}, {}
+        qs = {}
 
         def st_q(T):
-            b = T // TILES_PER_B
-            pexp, ssum = exps[T]
             q = work.tile([P, 8, N], F32, name="q", tag="q")
             nc.vector.scalar_tensor_tensor(
                 out=q[:].rearrange("p j i -> p (j i)"),
                 in0=pes[T][:],
                 scalar=besa[:, 0:1],
-                in1=pexp[:],
+                in1=exps[T][0][:],
                 op0=ALU.add,
                 op1=ALU.mult,
             )
             qs[T] = q
-            if T >= GPS_TILES:
-                rinv = small.tile([P, 8], F32, name="rinv", tag="rinv")
-                nc.vector.reciprocal(out=rinv[:], in_=ssum[:])
+
+        def st_norm_sum(T):
+            b, g = divmod(T, TILES_PER_B)
+            q = qs[T]
+            rinv = small.tile([P, 8], F32, name="rinv", tag="rinv")
+            nc.vector.reciprocal(out=rinv[:], in_=exps[T][1][:])
+            if T < GPS_TILES:
+                r_b = rinv[:].unsqueeze(2).to_broadcast([P, 8, N])
+                if g == 0:
+                    nc.gpsimd.tensor_tensor(out=acc8[:, b], in0=q[:], in1=r_b, op=ALU.mult)
+                else:
+                    wq = work.tile([P, 8, N], F32, name="wq", tag="wq")
+                    nc.gpsimd.tensor_tensor(out=wq[:], in0=q[:], in1=r_b, op=ALU.mult)
+                    nc.gpsimd.tensor_tensor(out=acc8[:, b], in0=acc8[:, b], in1=wq[:], op=ALU.add)
+            else:
                 for j in range(8):
                     nc.vector.scalar_tensor_tensor(
                         out=acc8[:, b, j, :],
@@ -276,24 +280,6 @@ def tile_languagemsgencoder_pb_t_kernel(
                         op0=ALU.mult,
                         op1=ALU.add,
                     )
-
-        def st_gps(T, half):
-            b, g = divmod(T, TILES_PER_B)
-            if half == 0:
-                rinvs[T] = small.tile([P, 8], F32, name="rinv", tag="rinv")
-            rinv = rinvs[T]
-            js = slice(4 * half, 4 * half + 4)
-            nc.vector.reciprocal(out=rinv[:, js], in_=exps[T][1][:, js])
-            r_b = rinv[:, js].unsqueeze(2).to_broadcast([P, 4, N])
-            q = qs[T]
-            if g == 0:
-                nc.gpsimd.tensor_tensor(out=acc8[:, b, js, :], in0=q[:, js, :], in1=r_b, op=ALU.mult)
-            else:
-                wq = work.tile([P, 4, N], F32, name="wq", tag="wq")
-                nc.gpsimd.tensor_tensor(out=wq[:], in0=q[:, js, :], in1=r_b, op=ALU.mult)
-                nc.gpsimd.tensor_tensor(
-                    out=acc8[:, b, js, :], in0=acc8[:, b, js, :], in1=wq[:], op=ALU.add
-                )
 
         def sum_partials(b):
             nc.vector.tensor_reduce(
@@ -323,14 +309,22 @@ def tile_languagemsgencoder_pb_t_kernel(
             out=xgw.rearrange("p (r c u) -> p r c u", r=2, u=2),
             in_=x_tr[:].rearrange("p r u c -> p r c u"),
         )
-        xrep = const.tile([P, 4 * B * 4 * N], BF16, name="xrep", align_bytes=64)
-        nc.vector.tensor_copy(
-            out=xrep[:].bitcast(F32).rearrange("p (b r w) -> p b r w", b=B, r=4),
-            in_=xgw.rearrange("p (b w) -> p b w", b=B).unsqueeze(2).to_broadcast([P, B, 4, 2 * N]),
-        )
-        wts["x"] = quantise(xg[:], B * N, "x")
+        x_c = const.tile([P, B * N], U32, name="x_c", align_bytes=64)
+        x_s = const.tile([P, B * N], U8, name="x_s", align_bytes=64)
+        nc.vector.memset(x_s[:].bitcast(I32), 0)
+        nc.vector.quantize_mx(out=x_c[:].bitcast(FP8X4), scales=x_s[:], in_=xg[:])
         gb_grp = regroup_stationary(gb_raw)
-        wts["xr"] = quantise(xrep[:], B * 4 * N, "xr")
+        xr_c = const.tile([P, B * 4 * N], U32, name="xr_c", align_bytes=64)
+        xr_s = const.tile([P, B * 4 * N], U8, name="xr_s", align_bytes=64)
+        nc.vector.tensor_copy(
+            out=xr_c[:].bitcast(I32).rearrange("p (b r w) -> p b r w", b=B, r=4),
+            in_=x_c[:].bitcast(I32).rearrange("p (b w) -> p b w", b=B).unsqueeze(2).to_broadcast([P, B, 4, N]),
+        )
+        nc.vector.tensor_copy(
+            out=xr_s[:].bitcast(I32).rearrange("p (b r w) -> p b r w", b=B, r=4),
+            in_=x_s[:].bitcast(I32).rearrange("p (b w) -> p b w", b=B).unsqueeze(2).to_broadcast([P, B, 4, N // 4]),
+        )
+        wts["xr"] = (xr_c, xr_s)
         gc_grp = regroup_stationary(gc_raw)
         wts["gb"] = quantise(gb_grp[:].rearrange("p a b c -> p (a b c)"), D, "gb")
         st_transpose(0)
@@ -338,10 +332,9 @@ def tile_languagemsgencoder_pb_t_kernel(
         st_transpose(1)
 
         bgr = const.tile([P, 4], F32, name="bgr")
-        nc.vector.tensor_copy(out=bgr[:], in_=bgr_bf[:])
-        nc.vector.tensor_copy(out=besa[:], in_=besa_bf[:])
+        nc.scalar.copy(out=bgr[:], in_=bgr_bf[:])
+        nc.scalar.copy(out=besa[:], in_=besa_bf[:])
         bb = const.tile([P, B, N // 2, 2, 4], F32, name="bb")
-        x_c, x_s = wts["x"]
         gb_c, gb_s = wts["gb"]
         pbs = []
         for h in range(2):
@@ -370,9 +363,12 @@ def tile_languagemsgencoder_pb_t_kernel(
         wts["bb"] = bb[:].rearrange("p b n jh t -> p b (n jh) t")
         wts["ga"] = quantise(ga_grp[:].rearrange("p a b c -> p (a b c)"), D, "ga")
 
-        def prepare_w_esa():
-            we_grp = const.tile([P, F, 4], BF16, name="we_grp", align_bytes=64)
-            nc.vector.tensor_copy(out=we_grp[:], in_=we_raw[:].rearrange("p t n -> p n t"))
+        we_grp = const.tile([P, F, 4], BF16, name="we_grp", align_bytes=64)
+
+        def regroup_w_esa():
+            nc.scalar.copy(out=we_grp[:], in_=we_raw[:].rearrange("p t n -> p n t"))
+
+        def quantise_w_esa():
             wts["we"] = quantise(we_grp[:].rearrange("p n t -> p (n t)"), F, "we")
 
         nxs = {}
@@ -411,10 +407,6 @@ def tile_languagemsgencoder_pb_t_kernel(
                 out=out_0.rearrange("b n d -> (b n) d")[P * r : P * r + P, :], in_=nxt[:]
             )
 
-        def gps(T, half):
-            if 0 <= T < GPS_TILES:
-                st_gps(T, half)
-
         def add_then_mx(T, ci):
             if live(T):
                 st_add(T, ci)
@@ -425,57 +417,60 @@ def tile_languagemsgencoder_pb_t_kernel(
             if live(T - 2):
                 st_q2(T - 2)
                 st_e(T - 2)
+            if live(T + 2):
+                st_q1(T + 2)
             if live(T - 3):
                 st_exp(T - 3)
-            gps(T - 4, 0)
+            if live(T - 4):
+                st_norm_sum(T - 4)
             add_then_mx(T, 0)
             if live(T - 3):
                 st_q(T - 3)
             add_then_mx(T, 1)
-            if live(T + 2):
-                st_q1(T + 2)
-            gps(T - 4, 1)
             add_then_mx(T, 2)
-            if T == 1:
-                prepare_w_esa()
             if live(T - 1):
                 st_tanh(T - 1)
             if live(T - 2):
                 st_negmax(T - 2)
             add_then_mx(T, 3)
+            if T == 1:
+                quantise_w_esa()
             if live(T + 3):
                 st_evac(T + 3)
             if T == 0:
+                regroup_w_esa()
                 nx_regroup()
             if live(T + 4):
                 st_transpose(T + 4)
 
         L = N_TILES - 1
+        st_tanh(L)
         st_q2(L - 1)
         st_e(L - 1)
-        st_exp(L - 2)
-        gps(L - 3, 0)
-        st_q(L - 2)
-        gps(L - 3, 1)
-        st_tanh(L)
         nx_quantise()
         nx_matmul(0)
         nx_matmul(1)
-        st_negmax(L - 1)
-        sum_partials(0)
+        st_exp(L - 2)
         st_q2(L)
         st_e(L)
+        st_norm_sum(L - 3)
+        st_negmax(L - 1)
+        st_q(L - 2)
+        st_norm_sum(L - 2)
         st_exp(L - 1)
+        st_negmax(L)
         nx_add(0)
         nx_tanh(0)
-        st_negmax(L)
         st_exp(L)
+        st_q(L - 1)
         nx_add(1)
         nx_tanh(1)
-        st_q(L - 1)
+        sum_partials(0)
         sum_partials(1)
         store_pair(0)
         sum_partials(2)
+        st_norm_sum(L - 1)
         st_q(L)
+        st_norm_sum(L)
         sum_partials(3)
         store_pair(1)

@@ -20,7 +20,8 @@ FLOPS = 2 * (3 * B * N * D * D + B * N * N * D * D + B * N * N * D * F)
 TILES_PER_B = 8
 N_TILES = B * TILES_PER_B
 CHUNKS = 4
-GPS_TILES = N_TILES - 2
+NX_PIECES, NX_FIRST, NX_EVERY = 8, 4, 3
+GPS_TILES = N_TILES - 3
 
 
 def tile_languagemsgencoder_pb_t_kernel(
@@ -52,24 +53,26 @@ def tile_languagemsgencoder_pb_t_kernel(
         rel_rows = rel_h.rearrange("b i j k -> b (i j) k")
         raw_chunks = {}
 
-        def load_chunk(c, pieces=1):
+        def load_rows(c, first, count):
             b, h = divmod(c, 4)
-            raw = rawp.tile([P, 8, D], BF16, name="raw", tag="raw")
-            src = rel_rows[b].rearrange("(p n) k -> p n k", n=32)
-            step = 8 // pieces
-            for s in range(pieces):
-                nc.sync.dma_start(
-                    out=raw[:, step * s : step * s + step, :],
-                    in_=src[:, 8 * h + step * s : 8 * h + step * s + step, :],
-                )
-            raw_chunks[c] = raw
+            nc.sync.dma_start(
+                out=raw_chunks[c][:, first : first + count, :],
+                in_=rel_rows[b].rearrange("(p n) k -> p n k", n=32)[:, 8 * h + first : 8 * h + first + count, :],
+            )
+
+        def load_chunk(c, now=True):
+            raw_chunks[c] = rawp.tile([P, 8, D], BF16, name="raw", tag="raw")
+            if now:
+                load_rows(c, 0, 8)
 
         bgr_bf = const.tile([P, 4], BF16, name="bgr_bf")
         besa_bf = const.tile([P, 1], BF16, name="besa_bf")
+        bgo_bf = const.tile([P, 4], BF16, name="bgo_bf")
         we_raw = const.tile([P, 4, F], BF16, name="we_raw")
         with nc.allow_non_contiguous_dma(reason="small per-partition bias loads"):
             nc.scalar.dma_start(out=bgr_bf[:], in_=b_gr.rearrange("(p t) -> p t", t=4))
             nc.scalar.dma_start(out=besa_bf[:], in_=b_esa.rearrange("(p t) -> p t", t=1))
+            nc.scalar.dma_start(out=bgo_bf[:], in_=b_go.rearrange("(p t) -> p t", t=4))
 
         x_raw = const.tile([P, 2, D], BF16, name="x_raw")
         nc.sync.dma_start(
@@ -77,15 +80,15 @@ def tile_languagemsgencoder_pb_t_kernel(
         )
         gb_raw = load_k_first(W_gr[D : 2 * D, :], "gb_raw")
         gc_raw = load_k_first(W_gr[2 * D : 3 * D, :], "gc_raw")
-        load_chunk(0, pieces=2)
+        load_chunk(0, now=False)
+        load_rows(0, 0, 4)
         ga_raw = load_k_first(W_gr[0:D, :], "ga_raw")
+        load_rows(0, 4, 4)
         load_chunk(1)
         nc.sync.dma_start(out=we_raw[:], in_=W_esa.rearrange("(p t) n -> p t n", t=4))
         go_raw = load_k_first(W_go, "go_raw")
         load_chunk(2)
         load_chunk(3)
-        bgo_bc = const.tile([P, D], BF16, name="bgo_bc")
-        nc.sync.dma_start(out=bgo_bc[:], in_=b_go.partition_broadcast(P))
 
         def quantise(grouped_flat, width, name):
             codes = const.tile([P, width], U32, name=name + "_c", align_bytes=64)
@@ -202,7 +205,10 @@ def tile_languagemsgencoder_pb_t_kernel(
         def st_e(T):
             c2, s2 = c2s[T]
             we_c, we_s = wts["we"]
-            pe = ps_e.tile([P, D], F32, name="pe", tag="pe")
+            if T == N_TILES - 1:
+                pe = ps_p.tile([P, D], F32, name="pe_last", tag="pp")
+            else:
+                pe = ps_e.tile([P, D], F32, name="pe", tag="pe")
             nc.tensor.matmul_mx(
                 out=pe[:],
                 lhsT=we_c[:].bitcast(FP8X4),
@@ -239,7 +245,7 @@ def tile_languagemsgencoder_pb_t_kernel(
                 )
             exps[T] = (pexp, ssum)
 
-        acc8 = const.tile([P, B, 8, N], F32, name="acc8")
+        acc8 = const.tile([P, 8, B, N], F32, name="acc8")
         osum = const.tile([P, B * N], F32, name="osum")
         besa = const.tile([P, 1], F32, name="besa")
 
@@ -265,18 +271,20 @@ def tile_languagemsgencoder_pb_t_kernel(
             if T < GPS_TILES:
                 r_b = rinv[:].unsqueeze(2).to_broadcast([P, 8, N])
                 if g == 0:
-                    nc.gpsimd.tensor_tensor(out=acc8[:, b], in0=q[:], in1=r_b, op=ALU.mult)
+                    nc.gpsimd.tensor_tensor(out=acc8[:, :, b, :], in0=q[:], in1=r_b, op=ALU.mult)
                 else:
                     wq = work.tile([P, 8, N], F32, name="wq", tag="wq")
                     nc.gpsimd.tensor_tensor(out=wq[:], in0=q[:], in1=r_b, op=ALU.mult)
-                    nc.gpsimd.tensor_tensor(out=acc8[:, b], in0=acc8[:, b], in1=wq[:], op=ALU.add)
+                    nc.gpsimd.tensor_tensor(
+                        out=acc8[:, :, b, :], in0=acc8[:, :, b, :], in1=wq[:], op=ALU.add
+                    )
             else:
                 for j in range(8):
                     nc.vector.scalar_tensor_tensor(
-                        out=acc8[:, b, j, :],
+                        out=acc8[:, j, b, :],
                         in0=q[:, j, :],
                         scalar=rinv[:, j : j + 1],
-                        in1=acc8[:, b, j, :],
+                        in1=acc8[:, j, b, :],
                         op0=ALU.mult,
                         op1=ALU.add,
                     )
@@ -284,16 +292,34 @@ def tile_languagemsgencoder_pb_t_kernel(
         def sum_partials(b):
             nc.vector.tensor_reduce(
                 out=osum[:, N * b : N * b + N],
-                in_=acc8[:, b].rearrange("p j i -> p i j"),
+                in_=acc8[:, :, b, :].rearrange("p j i -> p i j"),
                 axis=AX.X,
                 op=ALU.add,
             )
 
-        def store_pair(h):
-            pf = ps_tr.tile([P, 2, 2, P], F32, name="pf", tag="tr")
-            nc.tensor.transpose(pf[:, 0, 0, :], osum[:, P * h : P * h + P], ident[:])
+        pfs = {}
+
+        def transpose_pair(h):
+            pfs[h] = ps_tr.tile([P, 2, 2, P], F32, name="pf", tag="tr")
+            nc.tensor.transpose(pfs[h][:, 0, 0, :], osum[:, P * h : P * h + P], ident[:])
+
+        def sum_and_transpose_pair(h):
+            pfs[h] = ps_tr.tile([P, 2, 2, P], F32, name="pf", tag="tr")
+            for j in range(8):
+                nc.tensor.matmul(
+                    out=pfs[h][:, 0, 0, :],
+                    lhsT=acc8[:, j, 2 * h : 2 * h + 2, :].rearrange("p b i -> p (b i)"),
+                    rhs=ident[:],
+                    start=(j == 0),
+                    stop=(j == 7),
+                )
+
+        def store_pair(h, on_scalar=False):
             ot = work.tile([P, P], F32, name="ot", tag="ot")
-            nc.vector.tensor_copy(out=ot[:], in_=pf[:, 0, 0, :])
+            if on_scalar:
+                nc.scalar.copy(out=ot[:], in_=pfs[h][:, 0, 0, :])
+            else:
+                nc.vector.tensor_copy(out=ot[:], in_=pfs[h][:, 0, 0, :])
             nc.sync.dma_start(
                 out=out_1.rearrange("b i c -> (b i) c")[P * h : P * h + P, :], in_=ot[:]
             )
@@ -352,6 +378,8 @@ def tile_languagemsgencoder_pb_t_kernel(
             pbs.append(pb)
         ga_grp = regroup_stationary(ga_raw)
         wts["gc"] = quantise(gc_grp[:].rearrange("p a b c -> p (a b c)"), D, "gc")
+        st_q1(0)
+        wts["ga"] = quantise(ga_grp[:].rearrange("p a b c -> p (a b c)"), D, "ga")
         for b in range(B):
             h, bl = divmod(b, 2)
             nc.vector.tensor_tensor(
@@ -361,7 +389,6 @@ def tile_languagemsgencoder_pb_t_kernel(
                 op=ALU.add,
             )
         wts["bb"] = bb[:].rearrange("p b n jh t -> p b (n jh) t")
-        wts["ga"] = quantise(ga_grp[:].rearrange("p a b c -> p (a b c)"), D, "ga")
 
         we_grp = const.tile([P, F, 4], BF16, name="we_grp", align_bytes=64)
 
@@ -371,41 +398,63 @@ def tile_languagemsgencoder_pb_t_kernel(
         def quantise_w_esa():
             wts["we"] = quantise(we_grp[:].rearrange("p n t -> p (n t)"), F, "we")
 
+        go_grp = const.tile([P, 4, P, 4], BF16, name="go_grp", align_bytes=64)
+        bgo = const.tile([P, 4], F32, name="bgo")
+        nxt = const.tile([P, 4, B * N], F32, name="nxt")
         nxs = {}
 
-        go_grp = const.tile([P, D, 4], BF16, name="go_grp", align_bytes=64)
-
-        def nx_regroup():
-            nc.scalar.copy(out=go_grp[:], in_=go_raw[:].rearrange("p t c -> p c t"))
+        def nx_regroup(piece):
+            cols = slice(P // NX_PIECES * piece, P // NX_PIECES * (piece + 1))
+            nc.scalar.copy(
+                out=go_grp[:, :, cols, :],
+                in_=go_raw[:].rearrange("p t (pp tm) -> p tm pp t", tm=4)[:, :, cols, :],
+            )
 
         def nx_quantise():
-            wts["go"] = quantise(go_grp[:].rearrange("p c t -> p (c t)"), D, "go")
+            wts["go"] = quantise(go_grp[:].rearrange("p a b c -> p (a b c)"), D, "go")
 
-        def nx_matmul(r):
+        def nx_matmul():
             go_c, go_s = wts["go"]
-            px = ps_p.tile([P, D], F32, name="px", tag="pp")
-            nc.tensor.matmul_mx(
-                out=px[:],
-                lhsT=x_c[:, P * r : P * r + P].bitcast(FP8X4),
-                lhsT_scale=x_s[:, P * r : P * r + P],
-                rhs=go_c[:].bitcast(FP8X4),
-                rhs_scale=go_s[:],
-                start=True,
-                stop=True,
-            )
-            nxs[r] = px
+            for half in range(2):
+                px = ps_tr.tile([P, 2, B * N], F32, name="px", tag="tr")
+                for e in range(2):
+                    tm = 2 * half + e
+                    nc.tensor.matmul_mx(
+                        out=px[:, e, :],
+                        lhsT=go_c[:, P * tm : P * tm + P].bitcast(FP8X4),
+                        lhsT_scale=go_s[:, P * tm : P * tm + P],
+                        rhs=x_c[:].bitcast(FP8X4),
+                        rhs_scale=x_s[:],
+                        start=True,
+                        stop=True,
+                    )
+                nxs[half] = px
 
-        def nx_add(r):
-            nx = work.tile([P, D], F32, name="nx", tag="nx", bufs=2)
-            nc.vector.tensor_tensor(out=nx[:], in0=nxs[r][:], in1=bgo_bc[:], op=ALU.add)
-            nxs[r] = nx
+        def nx_tanh():
+            for tm in range(4):
+                nc.scalar.activation(
+                    out=nxt[:, tm, :],
+                    in_=nxs[tm // 2][:, tm % 2, :],
+                    func=ACTF.Tanh,
+                    bias=bgo[:, tm : tm + 1],
+                    scale=1.0,
+                )
 
-        def nx_tanh(r):
-            nxt = work.tile([P, D], F32, name="nxt", tag="nxt", bufs=2)
-            nc.scalar.activation(out=nxt[:], in_=nxs[r][:], func=ACTF.Tanh)
-            nc.sync.dma_start(
-                out=out_0.rearrange("b n d -> (b n) d")[P * r : P * r + P, :], in_=nxt[:]
-            )
+        def nx_transpose():
+            for r in range(2):
+                pt = ps_tr.tile([P, 4, P], F32, name="pt", tag="tr")
+                for tm in range(4):
+                    nc.tensor.transpose(pt[:, tm, :], nxt[:, tm, P * r : P * r + P], ident[:])
+                nxs[r] = pt
+
+        def nx_store():
+            for r in range(2):
+                nxo = work.tile([P, P, 4], F32, name="nxo", tag="nxo", bufs=2)
+                nc.scalar.copy(out=nxo[:], in_=nxs[r][:].rearrange("p tm pp -> p pp tm"))
+                nc.sync.dma_start(
+                    out=out_0.rearrange("b n d -> (b n) d")[P * r : P * r + P, :],
+                    in_=nxo[:].rearrange("p pp tm -> p (pp tm)"),
+                )
 
         def add_then_mx(T, ci):
             if live(T):
@@ -414,10 +463,11 @@ def tile_languagemsgencoder_pb_t_kernel(
                 st_mx(T + 1, ci)
 
         for T in range(-2, N_TILES):
+            early = T < 2
             if live(T - 2):
                 st_q2(T - 2)
                 st_e(T - 2)
-            if live(T + 2):
+            if live(T + 2) and T + 2 > 0 and not early:
                 st_q1(T + 2)
             if live(T - 3):
                 st_exp(T - 3)
@@ -427,6 +477,8 @@ def tile_languagemsgencoder_pb_t_kernel(
             if live(T - 3):
                 st_q(T - 3)
             add_then_mx(T, 1)
+            if live(T + 2) and T + 2 > 0 and early:
+                st_q1(T + 2)
             add_then_mx(T, 2)
             if live(T - 1):
                 st_tanh(T - 1)
@@ -435,42 +487,47 @@ def tile_languagemsgencoder_pb_t_kernel(
             add_then_mx(T, 3)
             if T == 1:
                 quantise_w_esa()
+            if T == N_TILES - 5:
+                nx_quantise()
             if live(T + 3):
                 st_evac(T + 3)
             if T == 0:
                 regroup_w_esa()
-                nx_regroup()
+                nc.scalar.copy(out=bgo[:], in_=bgo_bf[:])
+            if T >= NX_FIRST and (T - NX_FIRST) % NX_EVERY == 0 and (T - NX_FIRST) // NX_EVERY < NX_PIECES:
+                nx_regroup((T - NX_FIRST) // NX_EVERY)
             if live(T + 4):
                 st_transpose(T + 4)
+            if T == N_TILES - 4:
+                nx_matmul()
+            if T == N_TILES - 3:
+                nx_tanh()
+                nx_transpose()
+            if T == N_TILES - 2:
+                nx_store()
+                sum_and_transpose_pair(0)
+            if T == N_TILES - 1:
+                store_pair(0, on_scalar=True)
 
         L = N_TILES - 1
         st_tanh(L)
         st_q2(L - 1)
         st_e(L - 1)
-        nx_quantise()
-        nx_matmul(0)
-        nx_matmul(1)
+        sum_partials(2)
         st_exp(L - 2)
         st_q2(L)
         st_e(L)
         st_norm_sum(L - 3)
         st_negmax(L - 1)
-        st_q(L - 2)
-        st_norm_sum(L - 2)
         st_exp(L - 1)
         st_negmax(L)
-        nx_add(0)
-        nx_tanh(0)
         st_exp(L)
+        st_q(L - 2)
         st_q(L - 1)
-        nx_add(1)
-        nx_tanh(1)
-        sum_partials(0)
-        sum_partials(1)
-        store_pair(0)
-        sum_partials(2)
+        st_norm_sum(L - 2)
         st_norm_sum(L - 1)
         st_q(L)
         st_norm_sum(L)
         sum_partials(3)
+        transpose_pair(1)
         store_pair(1)

@@ -74,11 +74,11 @@ def tile_languagemsgencoder_pb_t_kernel(
             nc.scalar.dma_start(out=besa_bf[:], in_=b_esa.rearrange("(p t) -> p t", t=1))
             nc.scalar.dma_start(out=bgo_bf[:], in_=b_go.rearrange("(p t) -> p t", t=4))
 
+        gb_raw = load_k_first(W_gr[D : 2 * D, :], "gb_raw")
         x_raw = const.tile([P, 2, D], BF16, name="x_raw")
         nc.sync.dma_start(
             out=x_raw[:], in_=node_h.rearrange("b n k -> (b n) k").rearrange("(r p) k -> p r k", p=P)
         )
-        gb_raw = load_k_first(W_gr[D : 2 * D, :], "gb_raw")
         gc_raw = load_k_first(W_gr[2 * D : 3 * D, :], "gc_raw")
         load_chunk(0, now=False)
         load_rows(0, 0, 4)
@@ -329,6 +329,7 @@ def tile_languagemsgencoder_pb_t_kernel(
             xw = x_raw[:, r, :].bitcast(F32)
             for u in range(2):
                 nc.tensor.transpose(x_tr[:, r, u, :], xw[:, P * u : P * u + P], ident[:])
+        gb_grp = regroup_stationary(gb_raw)
         xg = const.tile([P, 4 * B * N], BF16, name="xg", align_bytes=64)
         xgw = xg[:].bitcast(F32)
         nc.vector.tensor_copy(
@@ -339,7 +340,6 @@ def tile_languagemsgencoder_pb_t_kernel(
         x_s = const.tile([P, B * N], U8, name="x_s", align_bytes=64)
         nc.vector.memset(x_s[:].bitcast(I32), 0)
         nc.vector.quantize_mx(out=x_c[:].bitcast(FP8X4), scales=x_s[:], in_=xg[:])
-        gb_grp = regroup_stationary(gb_raw)
         xr_c = const.tile([P, B * 4 * N], U32, name="xr_c", align_bytes=64)
         xr_s = const.tile([P, B * 4 * N], U8, name="xr_s", align_bytes=64)
         nc.vector.tensor_copy(

@@ -20,6 +20,7 @@ FLOPS = 2 * (3 * B * N * D * D + B * N * N * D * D + B * N * N * D * F)
 TILES_PER_B = 8
 N_TILES = B * TILES_PER_B
 CHUNKS = 4
+ADDED = 3
 NX_PIECES, NX_FIRST, NX_EVERY = 8, 4, 3
 GPS_TILES = N_TILES - 3
 
@@ -104,7 +105,7 @@ def tile_languagemsgencoder_pb_t_kernel(
             return grp
 
         trs, g1s, c1s, pps, a32s, g2s, c2s, pes, negs, exps = {}, {}, {}, {}, {}, {}, {}, {}, {}, {}
-        wts = {}
+        wts, gps = {}, {}
 
         def live(T):
             return 0 <= T < N_TILES
@@ -146,25 +147,23 @@ def tile_languagemsgencoder_pb_t_kernel(
             gc_c, gc_s = wts["gc"]
             ga_c, ga_s = wts["ga"]
             xr_c, xr_s = wts["xr"]
-            h, tp = divmod(ci, 2)
-            pp = ps_p.tile([P, 2, 2 * P], F32, name="pp", tag="pp")
-            for e in range(2):
-                tm = 2 * tp + e
+            pp = ps_p.tile([P, 4, P], F32, name="pp", tag="pp")
+            for tm in range(4):
                 nc.tensor.matmul_mx(
-                    out=pp[:, e, :],
+                    out=pp[:, tm, :],
                     lhsT=gc_c[:, P * tm : P * tm + P].bitcast(FP8X4),
                     lhsT_scale=gc_s[:, P * tm : P * tm + P],
-                    rhs=c1[:, 2 * P * h : 2 * P * h + 2 * P].bitcast(FP8X4),
-                    rhs_scale=s1[:, 2 * P * h : 2 * P * h + 2 * P],
+                    rhs=c1[:, P * ci : P * ci + P].bitcast(FP8X4),
+                    rhs_scale=s1[:, P * ci : P * ci + P],
                     start=True,
                     stop=False,
                 )
                 nc.tensor.matmul_mx(
-                    out=pp[:, e, :],
+                    out=pp[:, tm, :],
                     lhsT=ga_c[:, P * tm : P * tm + P].bitcast(FP8X4),
                     lhsT_scale=ga_s[:, P * tm : P * tm + P],
-                    rhs=xr_c[:, 2 * P * b : 2 * P * b + 2 * P].bitcast(FP8X4),
-                    rhs_scale=xr_s[:, 2 * P * b : 2 * P * b + 2 * P],
+                    rhs=xr_c[:, P * b : P * b + P].bitcast(FP8X4),
+                    rhs_scale=xr_s[:, P * b : P * b + P],
                     start=False,
                     stop=True,
                 )
@@ -172,29 +171,48 @@ def tile_languagemsgencoder_pb_t_kernel(
 
         def st_add(T, ci):
             b, g = divmod(T, TILES_PER_B)
-            h, tp = divmod(ci, 2)
             if ci == 0:
-                a32s[T] = work.tile([P, 2, 2, 2 * P, 2], F32, name="a32", tag="a32")
-            first = 2 * (CHUNKS * g + 2 * h)
+                a32s[T] = work.tile([P, ADDED, P, 4], F32, name="a32", tag="a32")
+            first = 2 * (CHUNKS * g + ci)
             nc.vector.tensor_tensor(
-                out=a32s[T][:, h, tp].rearrange("p (g i) e -> p g i e", g=4),
-                in0=pps[(T, ci)][:].rearrange("p e (g i) -> p g i e", g=4),
-                in1=wts["bb"][:, b, first : first + 4, 2 * tp : 2 * tp + 2]
-                .unsqueeze(2)
-                .to_broadcast([P, 4, N, 2]),
+                out=a32s[T][:, ci].rearrange("p (g i) t -> p g i t", g=2),
+                in0=pps[(T, ci)][:].rearrange("p t (g i) -> p g i t", g=2),
+                in1=wts["bb"][:, b, first : first + 2, :].unsqueeze(2).to_broadcast([P, 2, N, 4]),
                 op=ALU.add,
             )
 
+        def st_direct(T):
+            b, g = divmod(T, TILES_PER_B)
+            first = 2 * (CHUNKS * g + ADDED)
+            gp = work.tile([P, 4, P], BF16, name="gp", tag="gp")
+            for tm in range(4):
+                for k in range(2):
+                    nc.scalar.activation(
+                        out=gp[:, tm, N * k : N * k + N],
+                        in_=pps[(T, ADDED)][:, tm, N * k : N * k + N],
+                        func=ACTF.Tanh,
+                        bias=wts["bb"][:, b, first + k, tm : tm + 1],
+                        scale=1.0,
+                    )
+            gps[T] = gp
+
+        def st_interleave(T):
+            g2s[T] = work.tile([P, 4 * D], BF16, name="g2", tag="g2", bufs=4, align_bytes=64)
+            nc.gpsimd.tensor_scalar(
+                out=g2s[T][:, 4 * P * ADDED :].rearrange("p (w t) -> p w t", t=4),
+                in0=gps[T][:].rearrange("p t w -> p w t"),
+                scalar1=1.0,
+                scalar2=0.0,
+                op0=ALU.mult,
+                op1=ALU.add,
+            )
+
         def st_tanh(T):
-            g2 = work.tile([P, 4 * D], BF16, name="g2", tag="g2", align_bytes=64)
-            w = 4 * D // 2
-            for h in range(2):
-                nc.scalar.activation(
-                    out=g2[:, w * h : w * h + w].rearrange("p (w tp e) -> p w tp e", tp=2, e=2),
-                    in_=a32s[T][:, h].rearrange("p tp w e -> p w tp e"),
-                    func=ACTF.Tanh,
-                )
-            g2s[T] = g2
+            nc.scalar.activation(
+                out=g2s[T][:, : 4 * P * ADDED],
+                in_=a32s[T][:].rearrange("p c w t -> p (c w t)"),
+                func=ACTF.Tanh,
+            )
 
         def st_q2(T):
             c2 = work.tile([P, D], U32, name="c2", tag="c2", align_bytes=64)
@@ -340,15 +358,15 @@ def tile_languagemsgencoder_pb_t_kernel(
         x_s = const.tile([P, B * N], U8, name="x_s", align_bytes=64)
         nc.vector.memset(x_s[:].bitcast(I32), 0)
         nc.vector.quantize_mx(out=x_c[:].bitcast(FP8X4), scales=x_s[:], in_=xg[:])
-        xr_c = const.tile([P, B * 4 * N], U32, name="xr_c", align_bytes=64)
-        xr_s = const.tile([P, B * 4 * N], U8, name="xr_s", align_bytes=64)
+        xr_c = const.tile([P, B * 2 * N], U32, name="xr_c", align_bytes=64)
+        xr_s = const.tile([P, B * 2 * N], U8, name="xr_s", align_bytes=64)
         nc.vector.tensor_copy(
-            out=xr_c[:].bitcast(I32).rearrange("p (b r w) -> p b r w", b=B, r=4),
-            in_=x_c[:].bitcast(I32).rearrange("p (b w) -> p b w", b=B).unsqueeze(2).to_broadcast([P, B, 4, N]),
+            out=xr_c[:].bitcast(I32).rearrange("p (b r w) -> p b r w", b=B, r=2),
+            in_=x_c[:].bitcast(I32).rearrange("p (b w) -> p b w", b=B).unsqueeze(2).to_broadcast([P, B, 2, N]),
         )
         nc.vector.tensor_copy(
-            out=xr_s[:].bitcast(I32).rearrange("p (b r w) -> p b r w", b=B, r=4),
-            in_=x_s[:].bitcast(I32).rearrange("p (b w) -> p b w", b=B).unsqueeze(2).to_broadcast([P, B, 4, N // 4]),
+            out=xr_s[:].bitcast(I32).rearrange("p (b r w) -> p b r w", b=B, r=2),
+            in_=x_s[:].bitcast(I32).rearrange("p (b w) -> p b w", b=B).unsqueeze(2).to_broadcast([P, B, 2, N // 4]),
         )
         wts["xr"] = (xr_c, xr_s)
         gc_grp = regroup_stationary(gc_raw)
@@ -457,7 +475,7 @@ def tile_languagemsgencoder_pb_t_kernel(
                 )
 
         def add_then_mx(T, ci):
-            if live(T):
+            if live(T) and ci < ADDED:
                 st_add(T, ci)
             if live(T + 1):
                 st_mx(T + 1, ci)
@@ -471,8 +489,12 @@ def tile_languagemsgencoder_pb_t_kernel(
                 st_q1(T + 2)
             if live(T - 3):
                 st_exp(T - 3)
+            if live(T):
+                st_direct(T)
             if live(T - 4):
                 st_norm_sum(T - 4)
+            if live(T):
+                st_interleave(T)
             add_then_mx(T, 0)
             if live(T - 3):
                 st_q(T - 3)

@@ -20,7 +20,7 @@ FLOPS = 2 * (3 * B * N * D * D + B * N * N * D * D + B * N * N * D * F)
 TILES_PER_B = 8
 N_TILES = B * TILES_PER_B
 CHUNKS = 4
-ADDED = 3
+ADDED = 7
 NX_PIECES, NX_FIRST, NX_EVERY = 8, 4, 3
 GPS_TILES = N_TILES - 3
 
@@ -172,34 +172,33 @@ def tile_languagemsgencoder_pb_t_kernel(
         def st_add(T, ci):
             b, g = divmod(T, TILES_PER_B)
             if ci == 0:
-                a32s[T] = work.tile([P, ADDED, P, 4], F32, name="a32", tag="a32")
+                a32s[T] = work.tile([P, ADDED, N, 4], F32, name="a32", tag="a32")
             first = 2 * (CHUNKS * g + ci)
+            count = min(2, ADDED - 2 * ci)
             nc.vector.tensor_tensor(
-                out=a32s[T][:, ci].rearrange("p (g i) t -> p g i t", g=2),
-                in0=pps[(T, ci)][:].rearrange("p t (g i) -> p g i t", g=2),
-                in1=wts["bb"][:, b, first : first + 2, :].unsqueeze(2).to_broadcast([P, 2, N, 4]),
+                out=a32s[T][:, 2 * ci : 2 * ci + count],
+                in0=pps[(T, ci)][:].rearrange("p t (g i) -> p g i t", g=2)[:, :count],
+                in1=wts["bb"][:, b, first : first + count, :].unsqueeze(2).to_broadcast([P, count, N, 4]),
                 op=ALU.add,
             )
 
         def st_direct(T):
             b, g = divmod(T, TILES_PER_B)
-            first = 2 * (CHUNKS * g + ADDED)
-            gp = work.tile([P, 4, P], BF16, name="gp", tag="gp")
+            gp = work.tile([P, 4, N], BF16, name="gp", tag="gp")
             for tm in range(4):
-                for k in range(2):
-                    nc.scalar.activation(
-                        out=gp[:, tm, N * k : N * k + N],
-                        in_=pps[(T, ADDED)][:, tm, N * k : N * k + N],
-                        func=ACTF.Tanh,
-                        bias=wts["bb"][:, b, first + k, tm : tm + 1],
-                        scale=1.0,
-                    )
+                nc.scalar.activation(
+                    out=gp[:, tm, :],
+                    in_=pps[(T, CHUNKS - 1)][:, tm, N : 2 * N],
+                    func=ACTF.Tanh,
+                    bias=wts["bb"][:, b, 8 * g + ADDED, tm : tm + 1],
+                    scale=1.0,
+                )
             gps[T] = gp
 
         def st_interleave(T):
             g2s[T] = work.tile([P, 4 * D], BF16, name="g2", tag="g2", bufs=4, align_bytes=64)
             nc.gpsimd.tensor_scalar(
-                out=g2s[T][:, 4 * P * ADDED :].rearrange("p (w t) -> p w t", t=4),
+                out=g2s[T][:, 4 * N * ADDED :].rearrange("p (w t) -> p w t", t=4),
                 in0=gps[T][:].rearrange("p t w -> p w t"),
                 scalar1=1.0,
                 scalar2=0.0,
@@ -209,8 +208,8 @@ def tile_languagemsgencoder_pb_t_kernel(
 
         def st_tanh(T):
             nc.scalar.activation(
-                out=g2s[T][:, : 4 * P * ADDED],
-                in_=a32s[T][:].rearrange("p c w t -> p (c w t)"),
+                out=g2s[T][:, : 4 * N * ADDED],
+                in_=a32s[T][:].rearrange("p g i t -> p (g i t)"),
                 func=ACTF.Tanh,
             )
 
@@ -475,7 +474,7 @@ def tile_languagemsgencoder_pb_t_kernel(
                 )
 
         def add_then_mx(T, ci):
-            if live(T) and ci < ADDED:
+            if live(T):
                 st_add(T, ci)
             if live(T + 1):
                 st_mx(T + 1, ci)

@@ -147,23 +147,25 @@ def tile_languagemsgencoder_pb_t_kernel(
             gc_c, gc_s = wts["gc"]
             ga_c, ga_s = wts["ga"]
             xr_c, xr_s = wts["xr"]
-            pp = ps_p.tile([P, 4, P], F32, name="pp", tag="pp")
-            for tm in range(4):
+            h, tp = divmod(ci, 2)
+            pp = ps_p.tile([P, 2, 2 * P], F32, name="pp", tag="pp")
+            for e in range(2):
+                tm = 2 * tp + e
                 nc.tensor.matmul_mx(
-                    out=pp[:, tm, :],
+                    out=pp[:, e, :],
                     lhsT=gc_c[:, P * tm : P * tm + P].bitcast(FP8X4),
                     lhsT_scale=gc_s[:, P * tm : P * tm + P],
-                    rhs=c1[:, P * ci : P * ci + P].bitcast(FP8X4),
-                    rhs_scale=s1[:, P * ci : P * ci + P],
+                    rhs=c1[:, 2 * P * h : 2 * P * h + 2 * P].bitcast(FP8X4),
+                    rhs_scale=s1[:, 2 * P * h : 2 * P * h + 2 * P],
                     start=True,
                     stop=False,
                 )
                 nc.tensor.matmul_mx(
-                    out=pp[:, tm, :],
+                    out=pp[:, e, :],
                     lhsT=ga_c[:, P * tm : P * tm + P].bitcast(FP8X4),
                     lhsT_scale=ga_s[:, P * tm : P * tm + P],
-                    rhs=xr_c[:, P * b : P * b + P].bitcast(FP8X4),
-                    rhs_scale=xr_s[:, P * b : P * b + P],
+                    rhs=xr_c[:, 2 * P * b : 2 * P * b + 2 * P].bitcast(FP8X4),
+                    rhs_scale=xr_s[:, 2 * P * b : 2 * P * b + 2 * P],
                     start=False,
                     stop=True,
                 )
@@ -171,14 +173,17 @@ def tile_languagemsgencoder_pb_t_kernel(
 
         def st_add(T, ci):
             b, g = divmod(T, TILES_PER_B)
+            h, tp = divmod(ci, 2)
             if ci == 0:
-                a32s[T] = work.tile([P, ADDED, N, 4], F32, name="a32", tag="a32")
-            first = 2 * (CHUNKS * g + ci)
-            count = min(2, ADDED - 2 * ci)
+                a32s[T] = work.tile([P, 2, 2, 2 * P, 2], F32, name="a32", tag="a32")
+            first = 2 * (CHUNKS * g + 2 * h)
+            count = min(4, ADDED - 4 * h)
             nc.vector.tensor_tensor(
-                out=a32s[T][:, 2 * ci : 2 * ci + count],
-                in0=pps[(T, ci)][:].rearrange("p t (g i) -> p g i t", g=2)[:, :count],
-                in1=wts["bb"][:, b, first : first + count, :].unsqueeze(2).to_broadcast([P, count, N, 4]),
+                out=a32s[T][:, h, tp].rearrange("p (g i) e -> p g i e", g=4)[:, :count],
+                in0=pps[(T, ci)][:].rearrange("p e (g i) -> p g i e", g=4)[:, :count],
+                in1=wts["bb"][:, b, first : first + count, 2 * tp : 2 * tp + 2]
+                .unsqueeze(2)
+                .to_broadcast([P, count, N, 2]),
                 op=ALU.add,
             )
 
@@ -188,7 +193,7 @@ def tile_languagemsgencoder_pb_t_kernel(
             for tm in range(4):
                 nc.scalar.activation(
                     out=gp[:, tm, :],
-                    in_=pps[(T, CHUNKS - 1)][:, tm, N : 2 * N],
+                    in_=pps[(T, 2 + tm // 2)][:, tm % 2, 3 * N : 4 * N],
                     func=ACTF.Tanh,
                     bias=wts["bb"][:, b, 8 * g + ADDED, tm : tm + 1],
                     scale=1.0,
@@ -207,11 +212,13 @@ def tile_languagemsgencoder_pb_t_kernel(
             )
 
         def st_tanh(T):
-            nc.scalar.activation(
-                out=g2s[T][:, : 4 * N * ADDED],
-                in_=a32s[T][:].rearrange("p g i t -> p (g i t)"),
-                func=ACTF.Tanh,
-            )
+            for h in range(2):
+                w = N * min(4, ADDED - 4 * h)
+                nc.scalar.activation(
+                    out=g2s[T][:, 16 * N * h : 16 * N * h + 4 * w].rearrange("p (w tp e) -> p w tp e", tp=2, e=2),
+                    in_=a32s[T][:, h, :, :w].rearrange("p tp w e -> p w tp e"),
+                    func=ACTF.Tanh,
+                )
 
         def st_q2(T):
             c2 = work.tile([P, D], U32, name="c2", tag="c2", align_bytes=64)
@@ -357,15 +364,15 @@ def tile_languagemsgencoder_pb_t_kernel(
         x_s = const.tile([P, B * N], U8, name="x_s", align_bytes=64)
         nc.vector.memset(x_s[:].bitcast(I32), 0)
         nc.vector.quantize_mx(out=x_c[:].bitcast(FP8X4), scales=x_s[:], in_=xg[:])
-        xr_c = const.tile([P, B * 2 * N], U32, name="xr_c", align_bytes=64)
-        xr_s = const.tile([P, B * 2 * N], U8, name="xr_s", align_bytes=64)
+        xr_c = const.tile([P, B * 4 * N], U32, name="xr_c", align_bytes=64)
+        xr_s = const.tile([P, B * 4 * N], U8, name="xr_s", align_bytes=64)
         nc.vector.tensor_copy(
-            out=xr_c[:].bitcast(I32).rearrange("p (b r w) -> p b r w", b=B, r=2),
-            in_=x_c[:].bitcast(I32).rearrange("p (b w) -> p b w", b=B).unsqueeze(2).to_broadcast([P, B, 2, N]),
+            out=xr_c[:].bitcast(I32).rearrange("p (b r w) -> p b r w", b=B, r=4),
+            in_=x_c[:].bitcast(I32).rearrange("p (b w) -> p b w", b=B).unsqueeze(2).to_broadcast([P, B, 4, N]),
         )
         nc.vector.tensor_copy(
-            out=xr_s[:].bitcast(I32).rearrange("p (b r w) -> p b r w", b=B, r=2),
-            in_=x_s[:].bitcast(I32).rearrange("p (b w) -> p b w", b=B).unsqueeze(2).to_broadcast([P, B, 2, N // 4]),
+            out=xr_s[:].bitcast(I32).rearrange("p (b r w) -> p b r w", b=B, r=4),
+            in_=x_s[:].bitcast(I32).rearrange("p (b w) -> p b w", b=B).unsqueeze(2).to_broadcast([P, B, 4, N // 4]),
         )
         wts["xr"] = (xr_c, xr_s)
         gc_grp = regroup_stationary(gc_raw)

@@ -21,8 +21,8 @@ TILES_PER_B = 8
 N_TILES = B * TILES_PER_B
 CHUNKS = 4
 ADDED = 7
-NX_PIECES, NX_FIRST, NX_EVERY = 8, 4, 3
-GPS_TILES = N_TILES - 3
+NX_PIECES, NX_ROUNDS = 8, 4
+GPS_TILES = N_TILES - 4
 
 
 def tile_languagemsgencoder_pb_t_kernel(
@@ -103,6 +103,9 @@ def tile_languagemsgencoder_pb_t_kernel(
             nc.scalar.copy(out=grp[:, 2:4], in_=src[:, 2:4])
             nc.vector.tensor_copy(out=grp[:, 0:2], in_=src[:, 0:2])
             return grp
+
+        def gps_copy(out, src):
+            nc.gpsimd.tensor_scalar(out=out, in0=src, scalar1=1.0, scalar2=0.0, op0=ALU.mult, op1=ALU.add)
 
         trs, g1s, c1s, pps, a32s, g2s, c2s, pes, negs, exps = {}, {}, {}, {}, {}, {}, {}, {}, {}, {}
         wts, gps = {}, {}
@@ -202,13 +205,8 @@ def tile_languagemsgencoder_pb_t_kernel(
 
         def st_interleave(T):
             g2s[T] = work.tile([P, 4 * D], BF16, name="g2", tag="g2", bufs=4, align_bytes=64)
-            nc.gpsimd.tensor_scalar(
-                out=g2s[T][:, 4 * N * ADDED :].rearrange("p (w t) -> p w t", t=4),
-                in0=gps[T][:].rearrange("p t w -> p w t"),
-                scalar1=1.0,
-                scalar2=0.0,
-                op0=ALU.mult,
-                op1=ALU.add,
+            gps_copy(
+                g2s[T][:, 4 * N * ADDED :].rearrange("p (w t) -> p w t", t=4), gps[T][:].rearrange("p t w -> p w t")
             )
 
         def st_tanh(T):
@@ -229,10 +227,7 @@ def tile_languagemsgencoder_pb_t_kernel(
         def st_e(T):
             c2, s2 = c2s[T]
             we_c, we_s = wts["we"]
-            if T == N_TILES - 1:
-                pe = ps_p.tile([P, D], F32, name="pe_last", tag="pp")
-            else:
-                pe = ps_e.tile([P, D], F32, name="pe", tag="pe")
+            pe = ps_e.tile([P, D], F32, name="pe", tag="pe")
             nc.tensor.matmul_mx(
                 out=pe[:],
                 lhsT=we_c[:].bitcast(FP8X4),
@@ -270,7 +265,8 @@ def tile_languagemsgencoder_pb_t_kernel(
             exps[T] = (pexp, ssum)
 
         acc8 = const.tile([P, 8, B, N], F32, name="acc8")
-        osum = const.tile([P, B * N], F32, name="osum")
+        wlast = const.tile([P, N_TILES - GPS_TILES, 8, 2, N], F32, name="wlast")
+        nc.gpsimd.memset(wlast[:, :, :, 0, :], 0.0)
         besa = const.tile([P, 1], F32, name="besa")
 
         qs = {}
@@ -292,50 +288,30 @@ def tile_languagemsgencoder_pb_t_kernel(
             q = qs[T]
             rinv = small.tile([P, 8], F32, name="rinv", tag="rinv")
             nc.vector.reciprocal(out=rinv[:], in_=exps[T][1][:])
-            if T < GPS_TILES:
-                r_b = rinv[:].unsqueeze(2).to_broadcast([P, 8, N])
-                if g == 0:
-                    nc.gpsimd.tensor_tensor(out=acc8[:, :, b, :], in0=q[:], in1=r_b, op=ALU.mult)
-                else:
-                    wq = work.tile([P, 8, N], F32, name="wq", tag="wq")
-                    nc.gpsimd.tensor_tensor(out=wq[:], in0=q[:], in1=r_b, op=ALU.mult)
-                    nc.gpsimd.tensor_tensor(
-                        out=acc8[:, :, b, :], in0=acc8[:, :, b, :], in1=wq[:], op=ALU.add
-                    )
+            r_b = rinv[:].unsqueeze(2).to_broadcast([P, 8, N])
+            if g == 0:
+                nc.gpsimd.tensor_tensor(out=acc8[:, :, b, :], in0=q[:], in1=r_b, op=ALU.mult)
             else:
-                for j in range(8):
-                    nc.vector.scalar_tensor_tensor(
-                        out=acc8[:, j, b, :],
-                        in0=q[:, j, :],
-                        scalar=rinv[:, j : j + 1],
-                        in1=acc8[:, j, b, :],
-                        op0=ALU.mult,
-                        op1=ALU.add,
-                    )
-
-        def sum_partials(b):
-            nc.vector.tensor_reduce(
-                out=osum[:, N * b : N * b + N],
-                in_=acc8[:, :, b, :].rearrange("p j i -> p i j"),
-                axis=AX.X,
-                op=ALU.add,
-            )
+                wq = work.tile([P, 8, N], F32, name="wq", tag="wq")
+                nc.gpsimd.tensor_tensor(out=wq[:], in0=q[:], in1=r_b, op=ALU.mult)
+                nc.gpsimd.tensor_tensor(
+                    out=acc8[:, :, b, :], in0=acc8[:, :, b, :], in1=wq[:], op=ALU.add
+                )
 
         pfs = {}
 
-        def transpose_pair(h):
-            pfs[h] = ps_tr.tile([P, 2, 2, P], F32, name="pf", tag="tr")
-            nc.tensor.transpose(pfs[h][:, 0, 0, :], osum[:, P * h : P * h + P], ident[:])
-
-        def sum_and_transpose_pair(h):
-            pfs[h] = ps_tr.tile([P, 2, 2, P], F32, name="pf", tag="tr")
-            for j in range(8):
+        def add_transposed(h, rows, first, last):
+            if first:
+                pfs[h] = ps_tr.tile([P, 2, 2, P], F32, name="pf", tag="tr")
+            count = rows.shape[1]
+            for j in range(count):
                 nc.tensor.matmul(
                     out=pfs[h][:, 0, 0, :],
-                    lhsT=acc8[:, j, 2 * h : 2 * h + 2, :].rearrange("p b i -> p (b i)"),
+                    lhsT=rows[:, j].rearrange("p b i -> p (b i)"),
                     rhs=ident[:],
-                    start=(j == 0),
-                    stop=(j == 7),
+                    is_transpose=True,
+                    start=(first and j == 0),
+                    stop=(last and j == count - 1),
                 )
 
         def store_pair(h, on_scalar=False):
@@ -417,7 +393,7 @@ def tile_languagemsgencoder_pb_t_kernel(
         we_grp = const.tile([P, F, 4], BF16, name="we_grp", align_bytes=64)
 
         def regroup_w_esa():
-            nc.scalar.copy(out=we_grp[:], in_=we_raw[:].rearrange("p t n -> p n t"))
+            gps_copy(we_grp[:], we_raw[:].rearrange("p t n -> p n t"))
 
         def quantise_w_esa():
             wts["we"] = quantise(we_grp[:].rearrange("p n t -> p (n t)"), F, "we")
@@ -429,9 +405,9 @@ def tile_languagemsgencoder_pb_t_kernel(
 
         def nx_regroup(piece):
             cols = slice(P // NX_PIECES * piece, P // NX_PIECES * (piece + 1))
-            nc.scalar.copy(
-                out=go_grp[:, :, cols, :],
-                in_=go_raw[:].rearrange("p t (pp tm) -> p tm pp t", tm=4)[:, :, cols, :],
+            gps_copy(
+                go_grp[:, :, cols, :],
+                go_raw[:].rearrange("p t (pp tm) -> p tm pp t", tm=4)[:, :, cols, :],
             )
 
         def nx_quantise():
@@ -522,8 +498,9 @@ def tile_languagemsgencoder_pb_t_kernel(
             if T == 0:
                 regroup_w_esa()
                 nc.scalar.copy(out=bgo[:], in_=bgo_bf[:])
-            if T >= NX_FIRST and (T - NX_FIRST) % NX_EVERY == 0 and (T - NX_FIRST) // NX_EVERY < NX_PIECES:
-                nx_regroup((T - NX_FIRST) // NX_EVERY)
+            if 0 <= T < NX_ROUNDS:
+                for piece in range(NX_PIECES // NX_ROUNDS):
+                    nx_regroup(NX_PIECES // NX_ROUNDS * T + piece)
             if live(T + 4):
                 st_transpose(T + 4)
             if T == N_TILES - 4:
@@ -533,29 +510,123 @@ def tile_languagemsgencoder_pb_t_kernel(
                 nx_transpose()
             if T == N_TILES - 2:
                 nx_store()
-                sum_and_transpose_pair(0)
+                add_transposed(0, acc8[:, :, 0:2, :], first=True, last=True)
             if T == N_TILES - 1:
                 store_pair(0, on_scalar=True)
 
         L = N_TILES - 1
-        st_tanh(L)
+        halves = {}
+
+        def tanh_half(h):
+            w = N * min(4, ADDED - 4 * h)
+            nc.scalar.activation(
+                out=g2s[L][:, 16 * N * h : 16 * N * h + 4 * w].rearrange("p (w tp e) -> p w tp e", tp=2, e=2),
+                in_=a32s[L][:, h, :, :w].rearrange("p tp w e -> p w tp e"),
+                func=ACTF.Tanh,
+            )
+
+        def q2_e_half(h):
+            if h == 0:
+                c2 = work.tile([P, D], U32, name="c2", tag="c2", align_bytes=64)
+                s2 = work.tile([P, D], U8, name="s2", tag="s2", align_bytes=64)
+                pes[L] = ps_p.tile([P, D], F32, name="pe_last", tag="pp")
+                c2s[L] = (c2, s2)
+            c2, s2 = c2s[L]
+            we_c, we_s = wts["we"]
+            cols = slice(4 * N * h, 4 * N * h + 4 * N)
+            nc.vector.quantize_mx(
+                out=c2[:, cols].bitcast(FP8X4), scales=s2[:, cols], in_=g2s[L][:, 16 * N * h : 16 * N * h + 16 * N]
+            )
+            nc.tensor.matmul_mx(
+                out=pes[L][:, cols],
+                lhsT=we_c[:].bitcast(FP8X4),
+                lhsT_scale=we_s[:],
+                rhs=c2[:, cols].bitcast(FP8X4),
+                rhs_scale=s2[:, cols],
+                start=True,
+                stop=True,
+            )
+
+        def negmax_half(h):
+            negmax = small.tile([P, 4], F32, name="negmax_half", tag="negmax_half")
+            nc.vector.tensor_reduce(
+                out=negmax[:],
+                in_=pes[L][:, 4 * N * h : 4 * N * h + 4 * N].rearrange("p (j i) -> p j i", j=4),
+                axis=AX.X,
+                op=ALU.max,
+                negate=True,
+            )
+            halves[h] = [negmax]
+
+        def exp_half(h):
+            pexp = work.tile([P, 4, N], F32, name="pexp_half", tag="pexp_half", bufs=2)
+            ssum = small.tile([P, 4], F32, name="ssum_half", tag="ssum_half")
+            for j in range(4):
+                nc.scalar.activation(
+                    out=pexp[:, j, :],
+                    in_=pes[L][:, N * (4 * h + j) : N * (4 * h + j) + N],
+                    func=ACTF.Exp,
+                    bias=halves[h][0][:, j : j + 1],
+                    scale=1.0,
+                    accum_out=ssum[:, j : j + 1],
+                )
+            halves[h] += [pexp, ssum]
+
+        def q_half(h):
+            q = work.tile([P, 4, N], F32, name="q_half", tag="q_half", bufs=2)
+            nc.vector.scalar_tensor_tensor(
+                out=q[:].rearrange("p j i -> p (j i)"),
+                in0=pes[L][:, 4 * N * h : 4 * N * h + 4 * N],
+                scalar=besa[:, 0:1],
+                in1=halves[h][1][:].rearrange("p j i -> p (j i)"),
+                op0=ALU.add,
+                op1=ALU.mult,
+            )
+            rinv = small.tile([P, 4], F32, name="rinv_half", tag="rinv_half")
+            nc.vector.reciprocal(out=rinv[:], in_=halves[h][2][:])
+            halves[h] += [q, rinv]
+
+        def weigh(eng, T, first, q, rinv):
+            count = q[:].shape[1]
+            eng.tensor_tensor(
+                out=wlast[:, T - GPS_TILES, first : first + count, 1, :],
+                in0=q[:],
+                in1=rinv[:].unsqueeze(2).to_broadcast([P, count, N]),
+                op=ALU.mult,
+            )
+
+        def recip(T):
+            rinv = small.tile([P, 8], F32, name="rinv", tag="rinv")
+            nc.vector.reciprocal(out=rinv[:], in_=exps[T][1][:])
+            return rinv
+
+        tanh_half(0)
+        tanh_half(1)
         st_q2(L - 1)
         st_e(L - 1)
-        sum_partials(2)
+        q2_e_half(0)
         st_exp(L - 2)
-        st_q2(L)
-        st_e(L)
-        st_norm_sum(L - 3)
+        weigh(nc.gpsimd, L - 3, 0, qs[L - 3], recip(L - 3))
+        add_transposed(1, acc8[:, :, 2:4, :], first=True, last=False)
+        q2_e_half(1)
+        add_transposed(1, wlast[:, 0], first=False, last=False)
         st_negmax(L - 1)
         st_exp(L - 1)
-        st_negmax(L)
-        st_exp(L)
         st_q(L - 2)
+        weigh(nc.gpsimd, L - 2, 0, qs[L - 2], recip(L - 2))
+        negmax_half(0)
+        exp_half(0)
+        negmax_half(1)
+        exp_half(1)
+        add_transposed(1, wlast[:, 1], first=False, last=False)
         st_q(L - 1)
-        st_norm_sum(L - 2)
-        st_norm_sum(L - 1)
-        st_q(L)
-        st_norm_sum(L)
-        sum_partials(3)
-        transpose_pair(1)
+        r1 = recip(L - 1)
+        q_half(0)
+        weigh(nc.vector, L - 1, 0, qs[L - 1], r1)
+        q_half(1)
+        add_transposed(1, wlast[:, 2], first=False, last=False)
+        weigh(nc.vector, L, 0, halves[0][3], halves[0][4])
+        add_transposed(1, wlast[:, 3, 0:4], first=False, last=False)
+        weigh(nc.vector, L, 4, halves[1][3], halves[1][4])
+        add_transposed(1, wlast[:, 3, 4:8], first=False, last=True)
         store_pair(1)

@@ -20,7 +20,7 @@ FLOPS = 2 * (3 * B * N * D * D + B * N * N * D * D + B * N * N * D * F)
 TILES_PER_B = 8
 N_TILES = B * TILES_PER_B
 CHUNKS = 4
-ADDED = 7
+DIRECT = 2
 NX_PIECES, NX_ROUNDS = 8, 4
 GPS_TILES = N_TILES - 4
 
@@ -37,11 +37,19 @@ def tile_languagemsgencoder_pb_t_kernel(
         work = ctx.enter_context(tc.tile_pool(name="work", bufs=3))
         small = ctx.enter_context(tc.tile_pool(name="small", bufs=4))
         ps_tr = ctx.enter_context(tc.psum_pool(name="ps_tr", bufs=2))
-        ps_p = ctx.enter_context(tc.psum_pool(name="ps_p", bufs=4))
+        ps_p = ctx.enter_context(tc.psum_pool(name="ps_p", bufs=2))
+        ps_d = ctx.enter_context(tc.psum_pool(name="ps_d", bufs=1))
+        ps_o = ctx.enter_context(tc.psum_pool(name="ps_o", bufs=1))
         ps_e = ctx.enter_context(tc.psum_pool(name="ps_e", bufs=2))
 
         ident = const.tile([P, P], F32, name="ident")
         make_identity(nc, ident[:])
+        fold = const.tile([P, 2, P], F32, name="fold")
+        nc.gpsimd.memset(fold[:], 0.0)
+        for e in range(2):
+            nc.gpsimd.tensor_tensor(
+                out=fold[:, e, N * e : N * e + N], in0=ident[:, :N], in1=ident[:, N:], op=ALU.add
+            )
 
         def load_k_first(rows, name):
             raw = const.tile([P, 4, D], BF16, name=name)
@@ -150,25 +158,29 @@ def tile_languagemsgencoder_pb_t_kernel(
             gc_c, gc_s = wts["gc"]
             ga_c, ga_s = wts["ga"]
             xr_c, xr_s = wts["xr"]
-            h, tp = divmod(ci, 2)
-            pp = ps_p.tile([P, 2, 2 * P], F32, name="pp", tag="pp")
-            for e in range(2):
-                tm = 2 * tp + e
+            if ci < 2:
+                pp = ps_p.tile([P, 2, 2 * P], F32, name="pp", tag="pp")
+                tms, first, count = range(2 * ci, 2 * ci + 2), 0, 2 * P
+            else:
+                pool = ps_p if ci == 2 else ps_d
+                pp = pool.tile([P, 4, P], F32, name="pp", tag="pp")
+                tms, first, count = range(4), P * ci, P
+            for slot, tm in enumerate(tms):
                 nc.tensor.matmul_mx(
-                    out=pp[:, e, :],
+                    out=pp[:, slot, :],
                     lhsT=gc_c[:, P * tm : P * tm + P].bitcast(FP8X4),
                     lhsT_scale=gc_s[:, P * tm : P * tm + P],
-                    rhs=c1[:, 2 * P * h : 2 * P * h + 2 * P].bitcast(FP8X4),
-                    rhs_scale=s1[:, 2 * P * h : 2 * P * h + 2 * P],
+                    rhs=c1[:, first : first + count].bitcast(FP8X4),
+                    rhs_scale=s1[:, first : first + count],
                     start=True,
                     stop=False,
                 )
                 nc.tensor.matmul_mx(
-                    out=pp[:, e, :],
+                    out=pp[:, slot, :],
                     lhsT=ga_c[:, P * tm : P * tm + P].bitcast(FP8X4),
                     lhsT_scale=ga_s[:, P * tm : P * tm + P],
-                    rhs=xr_c[:, 2 * P * b : 2 * P * b + 2 * P].bitcast(FP8X4),
-                    rhs_scale=xr_s[:, 2 * P * b : 2 * P * b + 2 * P],
+                    rhs=xr_c[:, 2 * P * b : 2 * P * b + count].bitcast(FP8X4),
+                    rhs_scale=xr_s[:, 2 * P * b : 2 * P * b + count],
                     start=False,
                     stop=True,
                 )
@@ -176,45 +188,56 @@ def tile_languagemsgencoder_pb_t_kernel(
 
         def st_add(T, ci):
             b, g = divmod(T, TILES_PER_B)
-            h, tp = divmod(ci, 2)
             if ci == 0:
-                a32s[T] = work.tile([P, 2, 2, 2 * P, 2], F32, name="a32", tag="a32")
-            first = 2 * (CHUNKS * g + 2 * h)
-            count = min(4, ADDED - 4 * h)
+                a32s[T] = (
+                    work.tile([P, 2, 2 * P, 2], F32, name="a32", tag="a32"),
+                    work.tile([P, P, 4], F32, name="b32", tag="b32"),
+                )
+            if ci < 2:
+                out, groups, tms = a32s[T][0][:, ci], range(0, 4), slice(2 * ci, 2 * ci + 2)
+            else:
+                out, groups, tms = a32s[T][1][:], range(4, 6), slice(0, 4)
+            count = len(groups)
+            bb_t = wts["bb"][:, b, 8 * g + groups[0] : 8 * g + groups[0] + count, tms]
             nc.vector.tensor_tensor(
-                out=a32s[T][:, h, tp].rearrange("p (g i) e -> p g i e", g=4)[:, :count],
-                in0=pps[(T, ci)][:].rearrange("p e (g i) -> p g i e", g=4)[:, :count],
-                in1=wts["bb"][:, b, first : first + count, 2 * tp : 2 * tp + 2]
-                .unsqueeze(2)
-                .to_broadcast([P, count, N, 2]),
+                out=out.rearrange("p (g i) e -> p g i e", g=count),
+                in0=pps[(T, ci)][:].rearrange("p e (g i) -> p g i e", g=count),
+                in1=bb_t.unsqueeze(2).to_broadcast([P, count, N, tms.stop - tms.start]),
                 op=ALU.add,
             )
 
         def st_direct(T):
             b, g = divmod(T, TILES_PER_B)
-            gp = work.tile([P, 4, N], BF16, name="gp", tag="gp")
+            gp = work.tile([P, 4, DIRECT * N], BF16, name="gp", tag="gp")
             for tm in range(4):
-                nc.scalar.activation(
-                    out=gp[:, tm, :],
-                    in_=pps[(T, 2 + tm // 2)][:, tm % 2, 3 * N : 4 * N],
-                    func=ACTF.Tanh,
-                    bias=wts["bb"][:, b, 8 * g + ADDED, tm : tm + 1],
-                    scale=1.0,
-                )
+                for k in range(DIRECT):
+                    nc.scalar.activation(
+                        out=gp[:, tm, N * k : N * k + N],
+                        in_=pps[(T, 3)][:, tm, N * k : N * k + N],
+                        func=ACTF.Tanh,
+                        bias=wts["bb"][:, b, 8 * g + 8 - DIRECT + k, tm : tm + 1],
+                        scale=1.0,
+                    )
             gps[T] = gp
 
         def st_interleave(T):
             g2s[T] = work.tile([P, 4 * D], BF16, name="g2", tag="g2", bufs=4, align_bytes=64)
             gps_copy(
-                g2s[T][:, 4 * N * ADDED :].rearrange("p (w t) -> p w t", t=4), gps[T][:].rearrange("p t w -> p w t")
+                g2s[T][:, 4 * N * (8 - DIRECT) :].rearrange("p (w t) -> p w t", t=4),
+                gps[T][:].rearrange("p t w -> p w t"),
             )
 
-        def st_tanh(T):
-            for h in range(2):
-                w = N * min(4, ADDED - 4 * h)
+        def tanh_half(T, h):
+            if h == 0:
                 nc.scalar.activation(
-                    out=g2s[T][:, 16 * N * h : 16 * N * h + 4 * w].rearrange("p (w tp e) -> p w tp e", tp=2, e=2),
-                    in_=a32s[T][:, h, :, :w].rearrange("p tp w e -> p w tp e"),
+                    out=g2s[T][:, : 8 * P].rearrange("p (w tp e) -> p w tp e", tp=2, e=2),
+                    in_=a32s[T][0][:].rearrange("p tp w e -> p w tp e"),
+                    func=ACTF.Tanh,
+                )
+            else:
+                nc.scalar.activation(
+                    out=g2s[T][:, 8 * P : 12 * P],
+                    in_=a32s[T][1][:].rearrange("p w t -> p (w t)"),
                     func=ACTF.Tanh,
                 )
 
@@ -264,7 +287,7 @@ def tile_languagemsgencoder_pb_t_kernel(
                 )
             exps[T] = (pexp, ssum)
 
-        acc8 = const.tile([P, 8, B, N], F32, name="acc8")
+        accs = const.tile([P, B, F], F32, name="accs")
         wlast = const.tile([P, N_TILES - GPS_TILES, 8, 2, N], F32, name="wlast")
         nc.gpsimd.memset(wlast[:, :, :, 0, :], 0.0)
         besa = const.tile([P, 1], F32, name="besa")
@@ -283,26 +306,48 @@ def tile_languagemsgencoder_pb_t_kernel(
             )
             qs[T] = q
 
-        def st_norm_sum(T):
-            b, g = divmod(T, TILES_PER_B)
-            q = qs[T]
+        wqs, acc_banks = {}, {}
+
+        def st_norm(T):
             rinv = small.tile([P, 8], F32, name="rinv", tag="rinv")
             nc.vector.reciprocal(out=rinv[:], in_=exps[T][1][:])
-            r_b = rinv[:].unsqueeze(2).to_broadcast([P, 8, N])
+            wqs[T] = work.tile([P, 8, N], F32, name="wq", tag="wq")
+            nc.gpsimd.tensor_tensor(
+                out=wqs[T][:], in0=qs[T][:], in1=rinv[:].unsqueeze(2).to_broadcast([P, 8, N]), op=ALU.mult
+            )
+
+        def st_accumulate(T):
+            b, g = divmod(T, TILES_PER_B)
             if g == 0:
-                nc.gpsimd.tensor_tensor(out=acc8[:, :, b, :], in0=q[:], in1=r_b, op=ALU.mult)
-            else:
-                wq = work.tile([P, 8, N], F32, name="wq", tag="wq")
-                nc.gpsimd.tensor_tensor(out=wq[:], in0=q[:], in1=r_b, op=ALU.mult)
-                nc.gpsimd.tensor_tensor(
-                    out=acc8[:, :, b, :], in0=acc8[:, :, b, :], in1=wq[:], op=ALU.add
+                acc_banks[b] = ps_o.tile([P, F], F32, name="acc", tag="acc")
+            last = g == TILES_PER_B - 1 or T == GPS_TILES - 1
+            for k in range(4):
+                nc.tensor.matmul(
+                    out=acc_banks[b][:],
+                    lhsT=wqs[T][:, 2 * k : 2 * k + 2, :].rearrange("p j i -> p (j i)"),
+                    rhs=ident[:],
+                    is_transpose=True,
+                    start=(g == 0 and k == 0),
+                    stop=(last and k == 3),
                 )
+
+        def copy_sum(b):
+            nc.scalar.copy(out=accs[:, b, :], in_=acc_banks[b][:])
 
         pfs = {}
 
-        def add_transposed(h, rows, first, last):
-            if first:
-                pfs[h] = ps_tr.tile([P, 2, 2, P], F32, name="pf", tag="tr")
+        def fold_sums(h, last):
+            pfs[h] = ps_tr.tile([P, 2, 2, P], F32, name="pf", tag="tr")
+            for e in range(2):
+                nc.tensor.matmul(
+                    out=pfs[h][:, 0, 0, :],
+                    lhsT=fold[:, e, :],
+                    rhs=accs[:, 2 * h + e, :],
+                    start=(e == 0),
+                    stop=(last and e == 1),
+                )
+
+        def add_transposed(h, rows, last):
             count = rows.shape[1]
             for j in range(count):
                 nc.tensor.matmul(
@@ -310,7 +355,7 @@ def tile_languagemsgencoder_pb_t_kernel(
                     lhsT=rows[:, j].rearrange("p b i -> p (b i)"),
                     rhs=ident[:],
                     is_transpose=True,
-                    start=(first and j == 0),
+                    start=False,
                     stop=(last and j == count - 1),
                 )
 
@@ -459,8 +504,9 @@ def tile_languagemsgencoder_pb_t_kernel(
         def add_then_mx(T, ci):
             if live(T):
                 st_add(T, ci)
-            if live(T + 1):
-                st_mx(T + 1, ci)
+            Tm, cm = divmod(3 * T + ci + 2, 3)
+            if live(Tm):
+                st_mx(Tm, cm)
 
         for T in range(-2, N_TILES):
             early = T < 2
@@ -471,24 +517,28 @@ def tile_languagemsgencoder_pb_t_kernel(
                 st_q1(T + 2)
             if live(T - 3):
                 st_exp(T - 3)
+            if live(T - 5) and (T - 5) % TILES_PER_B == TILES_PER_B - 1:
+                copy_sum((T - 5) // TILES_PER_B)
             if live(T):
                 st_direct(T)
             if live(T - 4):
-                st_norm_sum(T - 4)
+                st_norm(T - 4)
             if live(T):
                 st_interleave(T)
             add_then_mx(T, 0)
             if live(T - 3):
                 st_q(T - 3)
             add_then_mx(T, 1)
+            if live(T + 1):
+                st_mx(T + 1, 3)
             if live(T + 2) and T + 2 > 0 and early:
                 st_q1(T + 2)
-            add_then_mx(T, 2)
             if live(T - 1):
-                st_tanh(T - 1)
+                for h in range(2):
+                    tanh_half(T - 1, h)
             if live(T - 2):
                 st_negmax(T - 2)
-            add_then_mx(T, 3)
+            add_then_mx(T, 2)
             if T == 1:
                 quantise_w_esa()
             if T == N_TILES - 5:
@@ -503,6 +553,8 @@ def tile_languagemsgencoder_pb_t_kernel(
                     nx_regroup(NX_PIECES // NX_ROUNDS * T + piece)
             if live(T + 4):
                 st_transpose(T + 4)
+            if live(T - 4):
+                st_accumulate(T - 4)
             if T == N_TILES - 4:
                 nx_matmul()
             if T == N_TILES - 3:
@@ -510,20 +562,12 @@ def tile_languagemsgencoder_pb_t_kernel(
                 nx_transpose()
             if T == N_TILES - 2:
                 nx_store()
-                add_transposed(0, acc8[:, :, 0:2, :], first=True, last=True)
+                fold_sums(0, last=True)
             if T == N_TILES - 1:
                 store_pair(0, on_scalar=True)
 
         L = N_TILES - 1
         halves = {}
-
-        def tanh_half(h):
-            w = N * min(4, ADDED - 4 * h)
-            nc.scalar.activation(
-                out=g2s[L][:, 16 * N * h : 16 * N * h + 4 * w].rearrange("p (w tp e) -> p w tp e", tp=2, e=2),
-                in_=a32s[L][:, h, :, :w].rearrange("p tp w e -> p w tp e"),
-                func=ACTF.Tanh,
-            )
 
         def q2_e_half(h):
             if h == 0:
@@ -600,16 +644,17 @@ def tile_languagemsgencoder_pb_t_kernel(
             nc.vector.reciprocal(out=rinv[:], in_=exps[T][1][:])
             return rinv
 
-        tanh_half(0)
-        tanh_half(1)
+        tanh_half(L, 0)
+        tanh_half(L, 1)
         st_q2(L - 1)
         st_e(L - 1)
         q2_e_half(0)
+        copy_sum(3)
         st_exp(L - 2)
         weigh(nc.gpsimd, L - 3, 0, qs[L - 3], recip(L - 3))
-        add_transposed(1, acc8[:, :, 2:4, :], first=True, last=False)
         q2_e_half(1)
-        add_transposed(1, wlast[:, 0], first=False, last=False)
+        fold_sums(1, last=False)
+        add_transposed(1, wlast[:, 0], last=False)
         st_negmax(L - 1)
         st_exp(L - 1)
         st_q(L - 2)
@@ -618,15 +663,15 @@ def tile_languagemsgencoder_pb_t_kernel(
         exp_half(0)
         negmax_half(1)
         exp_half(1)
-        add_transposed(1, wlast[:, 1], first=False, last=False)
+        add_transposed(1, wlast[:, 1], last=False)
         st_q(L - 1)
         r1 = recip(L - 1)
         q_half(0)
         weigh(nc.vector, L - 1, 0, qs[L - 1], r1)
         q_half(1)
-        add_transposed(1, wlast[:, 2], first=False, last=False)
+        add_transposed(1, wlast[:, 2], last=False)
         weigh(nc.vector, L, 0, halves[0][3], halves[0][4])
-        add_transposed(1, wlast[:, 3, 0:4], first=False, last=False)
+        add_transposed(1, wlast[:, 3, 0:4], last=False)
         weigh(nc.vector, L, 4, halves[1][3], halves[1][4])
-        add_transposed(1, wlast[:, 3, 4:8], first=False, last=True)
+        add_transposed(1, wlast[:, 3, 4:8], last=True)
         store_pair(1)

@@ -20,6 +20,7 @@ FLOPS = 2 * (3 * B * N * D * D + B * N * N * D * D + B * N * N * D * F)
 TILES_PER_B = 8
 N_TILES = B * TILES_PER_B
 CHUNKS = 4
+SHARE_FROM = 5
 DIRECT = 2
 NX_PIECES, NX_ROUNDS = 8, 4
 GPS_TILES = N_TILES - 4
@@ -135,16 +136,24 @@ def tile_languagemsgencoder_pb_t_kernel(
             if half == 1 and c + 4 < N_TILES // 2:
                 load_chunk(c + 4)
 
+        def evac(copy, T, pair, k):
+            if T not in g1s:
+                g1s[T] = work.tile([P, 4 * D], BF16, name="g1", tag="g1", align_bytes=64)
+            g1w = g1s[T][:].bitcast(F32).rearrange("p (c jh i u) -> p c jh i u", c=CHUNKS, jh=2, u=2)
+            copy(
+                out=g1w[:, 2 * pair + k],
+                in_=trs[T][pair][:, k].rearrange("p u (i jh) -> p jh i u", jh=2),
+            )
+
+        def st_evac_vector(T):
+            if T >= SHARE_FROM:
+                evac(nc.vector.tensor_copy, T, 1, 1)
+
         def st_evac(T):
-            g1 = work.tile([P, 4 * D], BF16, name="g1", tag="g1", align_bytes=64)
-            g1w = g1[:].bitcast(F32).rearrange("p (c jh i u) -> p c jh i u", c=CHUNKS, jh=2, u=2)
             for pair in range(2):
                 for k in range(2):
-                    nc.scalar.copy(
-                        out=g1w[:, 2 * pair + k],
-                        in_=trs[T][pair][:, k].rearrange("p u (i jh) -> p jh i u", jh=2),
-                    )
-            g1s[T] = g1
+                    if T < SHARE_FROM or (pair, k) != (1, 1):
+                        evac(nc.scalar.copy, T, pair, k)
 
         def st_q1(T):
             c1 = work.tile([P, D], U32, name="c1", tag="c1", align_bytes=64)
@@ -517,8 +526,6 @@ def tile_languagemsgencoder_pb_t_kernel(
                 st_q1(T + 2)
             if live(T - 3):
                 st_exp(T - 3)
-            if live(T - 5) and (T - 5) % TILES_PER_B == TILES_PER_B - 1:
-                copy_sum((T - 5) // TILES_PER_B)
             if live(T):
                 st_direct(T)
             if live(T - 4):
@@ -536,6 +543,8 @@ def tile_languagemsgencoder_pb_t_kernel(
             if live(T - 1):
                 for h in range(2):
                     tanh_half(T - 1, h)
+            if live(T + 3):
+                st_evac_vector(T + 3)
             if live(T - 2):
                 st_negmax(T - 2)
             add_then_mx(T, 2)
@@ -543,6 +552,8 @@ def tile_languagemsgencoder_pb_t_kernel(
                 quantise_w_esa()
             if T == N_TILES - 5:
                 nx_quantise()
+            if live(T - 5) and (T - 5) % TILES_PER_B == TILES_PER_B - 1:
+                copy_sum((T - 5) // TILES_PER_B)
             if live(T + 3):
                 st_evac(T + 3)
             if T == 0:

@@ -21,6 +21,7 @@ TILES_PER_B = 8
 N_TILES = B * TILES_PER_B
 CHUNKS = 4
 SHARE_FROM = 5
+VECTOR_ROWS = 48
 DIRECT = 2
 NX_PIECES, NX_ROUNDS = 8, 4
 GPS_TILES = N_TILES - 4
@@ -45,6 +46,8 @@ def tile_languagemsgencoder_pb_t_kernel(
 
         ident = const.tile([P, P], F32, name="ident")
         make_identity(nc, ident[:])
+        x_s = const.tile([P, B * N], U8, name="x_s", align_bytes=64)
+        nc.gpsimd.memset(x_s[:].bitcast(I32), 0)
         fold = const.tile([P, 2, P], F32, name="fold")
         nc.gpsimd.memset(fold[:], 0.0)
         for e in range(2):
@@ -106,11 +109,11 @@ def tile_languagemsgencoder_pb_t_kernel(
             nc.vector.quantize_mx(out=codes[:].bitcast(FP8X4), scales=plane[:], in_=grouped_flat)
             return codes, plane
 
-        def regroup_stationary(raw):
+        def regroup_stationary(raw, on_vector):
             grp = wtmp.tile([P, 4, P, 4], BF16, name="grp", tag="grp", bufs=3, align_bytes=64)
             src = raw[:].rearrange("p t (pp tm) -> p tm pp t", tm=4)
-            nc.scalar.copy(out=grp[:, 2:4], in_=src[:, 2:4])
-            nc.vector.tensor_copy(out=grp[:, 0:2], in_=src[:, 0:2])
+            nc.scalar.copy(out=grp[:, on_vector:], in_=src[:, on_vector:])
+            nc.vector.tensor_copy(out=grp[:, :on_vector], in_=src[:, :on_vector])
             return grp
 
         def gps_copy(out, src):
@@ -136,24 +139,24 @@ def tile_languagemsgencoder_pb_t_kernel(
             if half == 1 and c + 4 < N_TILES // 2:
                 load_chunk(c + 4)
 
-        def evac(copy, T, pair, k):
+        def evac(copy, T, pair, k, rows):
             if T not in g1s:
                 g1s[T] = work.tile([P, 4 * D], BF16, name="g1", tag="g1", align_bytes=64)
             g1w = g1s[T][:].bitcast(F32).rearrange("p (c jh i u) -> p c jh i u", c=CHUNKS, jh=2, u=2)
             copy(
-                out=g1w[:, 2 * pair + k],
-                in_=trs[T][pair][:, k].rearrange("p u (i jh) -> p jh i u", jh=2),
+                out=g1w[:, 2 * pair + k, :, rows],
+                in_=trs[T][pair][:, k].rearrange("p u (i jh) -> p jh i u", jh=2)[:, :, rows],
             )
 
         def st_evac_vector(T):
             if T >= SHARE_FROM:
-                evac(nc.vector.tensor_copy, T, 1, 1)
+                evac(nc.vector.tensor_copy, T, 1, 1, slice(0, VECTOR_ROWS))
 
         def st_evac(T):
             for pair in range(2):
                 for k in range(2):
-                    if T < SHARE_FROM or (pair, k) != (1, 1):
-                        evac(nc.scalar.copy, T, pair, k)
+                    shared = T >= SHARE_FROM and (pair, k) == (1, 1)
+                    evac(nc.scalar.copy, T, pair, k, slice(VECTOR_ROWS, N) if shared else slice(0, N))
 
         def st_q1(T):
             c1 = work.tile([P, D], U32, name="c1", tag="c1", align_bytes=64)
@@ -368,12 +371,9 @@ def tile_languagemsgencoder_pb_t_kernel(
                     stop=(last and j == count - 1),
                 )
 
-        def store_pair(h, on_scalar=False):
+        def store_pair(h):
             ot = work.tile([P, P], F32, name="ot", tag="ot")
-            if on_scalar:
-                nc.scalar.copy(out=ot[:], in_=pfs[h][:, 0, 0, :])
-            else:
-                nc.vector.tensor_copy(out=ot[:], in_=pfs[h][:, 0, 0, :])
+            nc.vector.tensor_copy(out=ot[:], in_=pfs[h][:, 0, 0, :])
             nc.sync.dma_start(
                 out=out_1.rearrange("b i c -> (b i) c")[P * h : P * h + P, :], in_=ot[:]
             )
@@ -383,7 +383,7 @@ def tile_languagemsgencoder_pb_t_kernel(
             xw = x_raw[:, r, :].bitcast(F32)
             for u in range(2):
                 nc.tensor.transpose(x_tr[:, r, u, :], xw[:, P * u : P * u + P], ident[:])
-        gb_grp = regroup_stationary(gb_raw)
+        gb_grp = regroup_stationary(gb_raw, 1)
         xg = const.tile([P, 4 * B * N], BF16, name="xg", align_bytes=64)
         xgw = xg[:].bitcast(F32)
         nc.vector.tensor_copy(
@@ -391,8 +391,6 @@ def tile_languagemsgencoder_pb_t_kernel(
             in_=x_tr[:].rearrange("p r u c -> p r c u"),
         )
         x_c = const.tile([P, B * N], U32, name="x_c", align_bytes=64)
-        x_s = const.tile([P, B * N], U8, name="x_s", align_bytes=64)
-        nc.vector.memset(x_s[:].bitcast(I32), 0)
         nc.vector.quantize_mx(out=x_c[:].bitcast(FP8X4), scales=x_s[:], in_=xg[:])
         xr_c = const.tile([P, B * 4 * N], U32, name="xr_c", align_bytes=64)
         xr_s = const.tile([P, B * 4 * N], U8, name="xr_s", align_bytes=64)
@@ -405,7 +403,7 @@ def tile_languagemsgencoder_pb_t_kernel(
             in_=x_s[:].bitcast(I32).rearrange("p (b w) -> p b w", b=B).unsqueeze(2).to_broadcast([P, B, 4, N // 4]),
         )
         wts["xr"] = (xr_c, xr_s)
-        gc_grp = regroup_stationary(gc_raw)
+        gc_grp = regroup_stationary(gc_raw, 1)
         wts["gb"] = quantise(gb_grp[:].rearrange("p a b c -> p (a b c)"), D, "gb")
         st_transpose(0)
         st_evac(0)
@@ -430,7 +428,7 @@ def tile_languagemsgencoder_pb_t_kernel(
                     stop=True,
                 )
             pbs.append(pb)
-        ga_grp = regroup_stationary(ga_raw)
+        ga_grp = regroup_stationary(ga_raw, 2)
         wts["gc"] = quantise(gc_grp[:].rearrange("p a b c -> p (a b c)"), D, "gc")
         st_q1(0)
         wts["ga"] = quantise(ga_grp[:].rearrange("p a b c -> p (a b c)"), D, "ga")
@@ -504,7 +502,7 @@ def tile_languagemsgencoder_pb_t_kernel(
         def nx_store():
             for r in range(2):
                 nxo = work.tile([P, P, 4], F32, name="nxo", tag="nxo", bufs=2)
-                nc.scalar.copy(out=nxo[:], in_=nxs[r][:].rearrange("p tm pp -> p pp tm"))
+                nc.vector.tensor_copy(out=nxo[:], in_=nxs[r][:].rearrange("p tm pp -> p pp tm"))
                 nc.sync.dma_start(
                     out=out_0.rearrange("b n d -> (b n) d")[P * r : P * r + P, :],
                     in_=nxo[:].rearrange("p pp tm -> p (pp tm)"),
@@ -575,7 +573,7 @@ def tile_languagemsgencoder_pb_t_kernel(
                 nx_store()
                 fold_sums(0, last=True)
             if T == N_TILES - 1:
-                store_pair(0, on_scalar=True)
+                store_pair(0)
 
         L = N_TILES - 1
         halves = {}

from contextlib import ExitStack

import concourse.mybir as mybir
from concourse.masks import make_identity

F32 = mybir.dt.float32
BF16 = mybir.dt.bfloat16
U32 = mybir.dt.uint32
U8 = mybir.dt.uint8
I32 = mybir.dt.int32
FP8X4 = mybir.dt.float8_e4m3fn_x4
ACTF = mybir.ActivationFunctionType
ALU = mybir.AluOpType
AX = mybir.AxisListType

P = 128
B, N, D, F = 4, 64, 512, 128
FLOPS = 2 * (3 * B * N * D * D + B * N * N * D * D + B * N * N * D * F)

TILES_PER_B = 8
N_TILES = B * TILES_PER_B
CHUNKS = 4
SHARE_FROM = 5
VECTOR_ROWS = 48
DIRECT = 2
NX_PIECES, NX_ROUNDS = 8, 4
GPS_TILES = N_TILES - 4


def tile_languagemsgencoder_pb_t_kernel(
    tc, node_h, rel_h, W_go, b_go, W_gr, b_gr, W_esa, b_esa, out_0, out_1
):
    nc = tc.nc
    with ExitStack() as ctx:
        ctx.enter_context(tc.manual_schedule())
        const = ctx.enter_context(tc.tile_pool(name="const", bufs=1))
        wtmp = ctx.enter_context(tc.tile_pool(name="wtmp", bufs=2))
        rawp = ctx.enter_context(tc.tile_pool(name="rawp", bufs=4))
        work = ctx.enter_context(tc.tile_pool(name="work", bufs=3))
        small = ctx.enter_context(tc.tile_pool(name="small", bufs=4))
        ps_tr = ctx.enter_context(tc.psum_pool(name="ps_tr", bufs=2))
        ps_p = ctx.enter_context(tc.psum_pool(name="ps_p", bufs=2))
        ps_d = ctx.enter_context(tc.psum_pool(name="ps_d", bufs=1))
        ps_o = ctx.enter_context(tc.psum_pool(name="ps_o", bufs=1))
        ps_e = ctx.enter_context(tc.psum_pool(name="ps_e", bufs=2))

        ident = const.tile([P, P], F32, name="ident")
        make_identity(nc, ident[:])
        x_s = const.tile([P, B * N], U8, name="x_s", align_bytes=64)
        nc.gpsimd.memset(x_s[:].bitcast(I32), 0)
        fold = const.tile([P, 2, P], F32, name="fold")
        nc.gpsimd.memset(fold[:], 0.0)
        for e in range(2):
            nc.gpsimd.tensor_tensor(
                out=fold[:, e, N * e : N * e + N], in0=ident[:, :N], in1=ident[:, N:], op=ALU.add
            )

        def load_k_first(rows, name):
            raw = const.tile([P, 4, D], BF16, name=name)
            nc.sync.dma_start(
                out=raw[:].rearrange("p (u e) c -> p u (e c)", u=2),
                in_=rows.rearrange("(u q e) c -> q u (e c)", u=2, e=2),
            )
            return raw

        rel_rows = rel_h.rearrange("b i j k -> b (i j) k")
        raw_chunks = {}

        def load_rows(c, first, count):
            b, h = divmod(c, 4)
            nc.sync.dma_start(
                out=raw_chunks[c][:, first : first + count, :],
                in_=rel_rows[b].rearrange("(p n) k -> p n k", n=32)[:, 8 * h + first : 8 * h + first + count, :],
            )

        def load_chunk(c, now=True):
            raw_chunks[c] = rawp.tile([P, 8, D], BF16, name="raw", tag="raw")
            if now:
                load_rows(c, 0, 8)

        bgr_bf = const.tile([P, 4], BF16, name="bgr_bf")
        besa_bf = const.tile([P, 1], BF16, name="besa_bf")
        bgo_bf = const.tile([P, 4], BF16, name="bgo_bf")
        we_raw = const.tile([P, 4, F], BF16, name="we_raw")
        with nc.allow_non_contiguous_dma(reason="small per-partition bias loads"):
            nc.scalar.dma_start(out=bgr_bf[:], in_=b_gr.rearrange("(p t) -> p t", t=4))
            nc.scalar.dma_start(out=besa_bf[:], in_=b_esa.rearrange("(p t) -> p t", t=1))
            nc.scalar.dma_start(out=bgo_bf[:], in_=b_go.rearrange("(p t) -> p t", t=4))

        gb_raw = load_k_first(W_gr[D : 2 * D, :], "gb_raw")
        x_raw = const.tile([P, 2, D], BF16, name="x_raw")
        nc.sync.dma_start(
            out=x_raw[:], in_=node_h.rearrange("b n k -> (b n) k").rearrange("(r p) k -> p r k", p=P)
        )
        gc_raw = load_k_first(W_gr[2 * D : 3 * D, :], "gc_raw")
        load_chunk(0, now=False)
        load_rows(0, 0, 4)
        ga_raw = load_k_first(W_gr[0:D, :], "ga_raw")
        load_rows(0, 4, 4)
        load_chunk(1)
        nc.sync.dma_start(out=we_raw[:], in_=W_esa.rearrange("(p t) n -> p t n", t=4))
        go_raw = load_k_first(W_go, "go_raw")
        load_chunk(2)
        load_chunk(3)

        def quantise(grouped_flat, width, name):
            codes = const.tile([P, width], U32, name=name + "_c", align_bytes=64)
            plane = const.tile([P, width], U8, name=name + "_s", align_bytes=64)
            nc.vector.quantize_mx(out=codes[:].bitcast(FP8X4), scales=plane[:], in_=grouped_flat)
            return codes, plane

        def regroup_stationary(raw, on_vector):
            grp = wtmp.tile([P, 4, P, 4], BF16, name="grp", tag="grp", bufs=3, align_bytes=64)
            src = raw[:].rearrange("p t (pp tm) -> p tm pp t", tm=4)
            nc.scalar.copy(out=grp[:, on_vector:], in_=src[:, on_vector:])
            nc.vector.tensor_copy(out=grp[:, :on_vector], in_=src[:, :on_vector])
            return grp

        def gps_copy(out, src):
            nc.gpsimd.tensor_scalar(out=out, in0=src, scalar1=1.0, scalar2=0.0, op0=ALU.mult, op1=ALU.add)

        trs, g1s, c1s, pps, a32s, g2s, c2s, pes, negs, exps = {}, {}, {}, {}, {}, {}, {}, {}, {}, {}
        wts, gps = {}, {}

        def live(T):
            return 0 <= T < N_TILES

        def st_transpose(T):
            c, half = divmod(T, 2)
            raw = raw_chunks[c]
            trs[T] = []
            for pair in range(2):
                tr = ps_tr.tile([P, 2, 2, P], F32, name="tr", tag="tr")
                for k in range(2):
                    rw = raw[:, 4 * half + 2 * pair + k, :].bitcast(F32)
                    for u in range(2):
                        nc.tensor.transpose(tr[:, k, u, :], rw[:, P * u : P * u + P], ident[:])
                trs[T].append(tr)
            if half == 1 and c + 4 < N_TILES // 2:
                load_chunk(c + 4)

        def evac(copy, T, pair, k, rows):
            if T not in g1s:
                g1s[T] = work.tile([P, 4 * D], BF16, name="g1", tag="g1", align_bytes=64)
            g1w = g1s[T][:].bitcast(F32).rearrange("p (c jh i u) -> p c jh i u", c=CHUNKS, jh=2, u=2)
            copy(
                out=g1w[:, 2 * pair + k, :, rows],
                in_=trs[T][pair][:, k].rearrange("p u (i jh) -> p jh i u", jh=2)[:, :, rows],
            )

        def st_evac_vector(T):
            if T >= SHARE_FROM:
                evac(nc.vector.tensor_copy, T, 1, 1, slice(0, VECTOR_ROWS))

        def st_evac(T):
            for pair in range(2):
                for k in range(2):
                    shared = T >= SHARE_FROM and (pair, k) == (1, 1)
                    evac(nc.scalar.copy, T, pair, k, slice(VECTOR_ROWS, N) if shared else slice(0, N))

        def st_q1(T):
            c1 = work.tile([P, D], U32, name="c1", tag="c1", align_bytes=64)
            s1 = work.tile([P, D], U8, name="s1", tag="s1", align_bytes=64)
            nc.vector.quantize_mx(out=c1[:].bitcast(FP8X4), scales=s1[:], in_=g1s[T][:])
            c1s[T] = (c1, s1)

        def st_mx(T, ci):
            b = T // TILES_PER_B
            c1, s1 = c1s[T]
            gc_c, gc_s = wts["gc"]
            ga_c, ga_s = wts["ga"]
            xr_c, xr_s = wts["xr"]
            if ci < 2:
                pp = ps_p.tile([P, 2, 2 * P], F32, name="pp", tag="pp")
                tms, first, count = range(2 * ci, 2 * ci + 2), 0, 2 * P
            else:
                pool = ps_p if ci == 2 else ps_d
                pp = pool.tile([P, 4, P], F32, name="pp", tag="pp")
                tms, first, count = range(4), P * ci, P
            for slot, tm in enumerate(tms):
                nc.tensor.matmul_mx(
                    out=pp[:, slot, :],
                    lhsT=gc_c[:, P * tm : P * tm + P].bitcast(FP8X4),
                    lhsT_scale=gc_s[:, P * tm : P * tm + P],
                    rhs=c1[:, first : first + count].bitcast(FP8X4),
                    rhs_scale=s1[:, first : first + count],
                    start=True,
                    stop=False,
                )
                nc.tensor.matmul_mx(
                    out=pp[:, slot, :],
                    lhsT=ga_c[:, P * tm : P * tm + P].bitcast(FP8X4),
                    lhsT_scale=ga_s[:, P * tm : P * tm + P],
                    rhs=xr_c[:, 2 * P * b : 2 * P * b + count].bitcast(FP8X4),
                    rhs_scale=xr_s[:, 2 * P * b : 2 * P * b + count],
                    start=False,
                    stop=True,
                )
            pps[(T, ci)] = pp

        def st_add(T, ci):
            b, g = divmod(T, TILES_PER_B)
            if ci == 0:
                a32s[T] = (
                    work.tile([P, 2, 2 * P, 2], F32, name="a32", tag="a32"),
                    work.tile([P, P, 4], F32, name="b32", tag="b32"),
                )
            if ci < 2:
                out, groups, tms = a32s[T][0][:, ci], range(0, 4), slice(2 * ci, 2 * ci + 2)
            else:
                out, groups, tms = a32s[T][1][:], range(4, 6), slice(0, 4)
            count = len(groups)
            bb_t = wts["bb"][:, b, 8 * g + groups[0] : 8 * g + groups[0] + count, tms]
            nc.vector.tensor_tensor(
                out=out.rearrange("p (g i) e -> p g i e", g=count),
                in0=pps[(T, ci)][:].rearrange("p e (g i) -> p g i e", g=count),
                in1=bb_t.unsqueeze(2).to_broadcast([P, count, N, tms.stop - tms.start]),
                op=ALU.add,
            )

        def st_direct(T):
            b, g = divmod(T, TILES_PER_B)
            gp = work.tile([P, 4, DIRECT * N], BF16, name="gp", tag="gp")
            for tm in range(4):
                for k in range(DIRECT):
                    nc.scalar.activation(
                        out=gp[:, tm, N * k : N * k + N],
                        in_=pps[(T, 3)][:, tm, N * k : N * k + N],
                        func=ACTF.Tanh,
                        bias=wts["bb"][:, b, 8 * g + 8 - DIRECT + k, tm : tm + 1],
                        scale=1.0,
                    )
            gps[T] = gp

        def st_interleave(T):
            g2s[T] = work.tile([P, 4 * D], BF16, name="g2", tag="g2", bufs=4, align_bytes=64)
            gps_copy(
                g2s[T][:, 4 * N * (8 - DIRECT) :].rearrange("p (w t) -> p w t", t=4),
                gps[T][:].rearrange("p t w -> p w t"),
            )

        def tanh_half(T, h):
            if h == 0:
                nc.scalar.activation(
                    out=g2s[T][:, : 8 * P].rearrange("p (w tp e) -> p w tp e", tp=2, e=2),
                    in_=a32s[T][0][:].rearrange("p tp w e -> p w tp e"),
                    func=ACTF.Tanh,
                )
            else:
                nc.scalar.activation(
                    out=g2s[T][:, 8 * P : 12 * P],
                    in_=a32s[T][1][:].rearrange("p w t -> p (w t)"),
                    func=ACTF.Tanh,
                )

        def st_q2(T):
            c2 = work.tile([P, D], U32, name="c2", tag="c2", align_bytes=64)
            s2 = work.tile([P, D], U8, name="s2", tag="s2", align_bytes=64)
            nc.vector.quantize_mx(out=c2[:].bitcast(FP8X4), scales=s2[:], in_=g2s[T][:])
            c2s[T] = (c2, s2)

        def st_e(T):
            c2, s2 = c2s[T]
            we_c, we_s = wts["we"]
            pe = ps_e.tile([P, D], F32, name="pe", tag="pe")
            nc.tensor.matmul_mx(
                out=pe[:],
                lhsT=we_c[:].bitcast(FP8X4),
                lhsT_scale=we_s[:],
                rhs=c2[:].bitcast(FP8X4),
                rhs_scale=s2[:],
                start=True,
                stop=True,
            )
            pes[T] = pe

        def st_negmax(T):
            negmax = small.tile([P, 8], F32, name="negmax", tag="negmax")
            nc.vector.tensor_reduce(
                out=negmax[:],
                in_=pes[T][:].rearrange("p (j i) -> p j i", j=8),
                axis=AX.X,
                op=ALU.max,
                negate=True,
            )
            negs[T] = negmax

        def st_exp(T):
            pexp = work.tile([P, D], F32, name="pexp", tag="pexp")
            ssum = small.tile([P, 8], F32, name="ssum", tag="ssum")
            for j in range(8):
                nc.scalar.activation(
                    out=pexp[:, N * j : N * j + N],
                    in_=pes[T][:, N * j : N * j + N],
                    func=ACTF.Exp,
                    bias=negs[T][:, j : j + 1],
                    scale=1.0,
                    accum_out=ssum[:, j : j + 1],
                )
            exps[T] = (pexp, ssum)

        accs = const.tile([P, B, F], F32, name="accs")
        wlast = const.tile([P, N_TILES - GPS_TILES, 8, 2, N], F32, name="wlast")
        nc.gpsimd.memset(wlast[:, :, :, 0, :], 0.0)
        besa = const.tile([P, 1], F32, name="besa")

        qs = {}

        def st_q(T):
            q = work.tile([P, 8, N], F32, name="q", tag="q")
            nc.vector.scalar_tensor_tensor(
                out=q[:].rearrange("p j i -> p (j i)"),
                in0=pes[T][:],
                scalar=besa[:, 0:1],
                in1=exps[T][0][:],
                op0=ALU.add,
                op1=ALU.mult,
            )
            qs[T] = q

        wqs, acc_banks = {}, {}

        def st_norm(T):
            rinv = small.tile([P, 8], F32, name="rinv", tag="rinv")
            nc.vector.reciprocal(out=rinv[:], in_=exps[T][1][:])
            wqs[T] = work.tile([P, 8, N], F32, name="wq", tag="wq")
            nc.gpsimd.tensor_tensor(
                out=wqs[T][:], in0=qs[T][:], in1=rinv[:].unsqueeze(2).to_broadcast([P, 8, N]), op=ALU.mult
            )

        def st_accumulate(T):
            b, g = divmod(T, TILES_PER_B)
            if g == 0:
                acc_banks[b] = ps_o.tile([P, F], F32, name="acc", tag="acc")
            last = g == TILES_PER_B - 1 or T == GPS_TILES - 1
            for k in range(4):
                nc.tensor.matmul(
                    out=acc_banks[b][:],
                    lhsT=wqs[T][:, 2 * k : 2 * k + 2, :].rearrange("p j i -> p (j i)"),
                    rhs=ident[:],
                    is_transpose=True,
                    start=(g == 0 and k == 0),
                    stop=(last and k == 3),
                )

        def copy_sum(b):
            nc.scalar.copy(out=accs[:, b, :], in_=acc_banks[b][:])

        pfs = {}

        def fold_sums(h, last):
            pfs[h] = ps_tr.tile([P, 2, 2, P], F32, name="pf", tag="tr")
            for e in range(2):
                nc.tensor.matmul(
                    out=pfs[h][:, 0, 0, :],
                    lhsT=fold[:, e, :],
                    rhs=accs[:, 2 * h + e, :],
                    start=(e == 0),
                    stop=(last and e == 1),
                )

        def add_transposed(h, rows, last):
            count = rows.shape[1]
            for j in range(count):
                nc.tensor.matmul(
                    out=pfs[h][:, 0, 0, :],
                    lhsT=rows[:, j].rearrange("p b i -> p (b i)"),
                    rhs=ident[:],
                    is_transpose=True,
                    start=False,
                    stop=(last and j == count - 1),
                )

        def store_pair(h):
            ot = work.tile([P, P], F32, name="ot", tag="ot")
            nc.vector.tensor_copy(out=ot[:], in_=pfs[h][:, 0, 0, :])
            nc.sync.dma_start(
                out=out_1.rearrange("b i c -> (b i) c")[P * h : P * h + P, :], in_=ot[:]
            )

        x_tr = ps_tr.tile([P, 2, 2, P], F32, name="x_tr", tag="tr")
        for r in range(2):
            xw = x_raw[:, r, :].bitcast(F32)
            for u in range(2):
                nc.tensor.transpose(x_tr[:, r, u, :], xw[:, P * u : P * u + P], ident[:])
        gb_grp = regroup_stationary(gb_raw, 1)
        xg = const.tile([P, 4 * B * N], BF16, name="xg", align_bytes=64)
        xgw = xg[:].bitcast(F32)
        nc.vector.tensor_copy(
            out=xgw.rearrange("p (r c u) -> p r c u", r=2, u=2),
            in_=x_tr[:].rearrange("p r u c -> p r c u"),
        )
        x_c = const.tile([P, B * N], U32, name="x_c", align_bytes=64)
        nc.vector.quantize_mx(out=x_c[:].bitcast(FP8X4), scales=x_s[:], in_=xg[:])
        xr_c = const.tile([P, B * 4 * N], U32, name="xr_c", align_bytes=64)
        xr_s = const.tile([P, B * 4 * N], U8, name="xr_s", align_bytes=64)
        nc.vector.tensor_copy(
            out=xr_c[:].bitcast(I32).rearrange("p (b r w) -> p b r w", b=B, r=4),
            in_=x_c[:].bitcast(I32).rearrange("p (b w) -> p b w", b=B).unsqueeze(2).to_broadcast([P, B, 4, N]),
        )
        nc.vector.tensor_copy(
            out=xr_s[:].bitcast(I32).rearrange("p (b r w) -> p b r w", b=B, r=4),
            in_=x_s[:].bitcast(I32).rearrange("p (b w) -> p b w", b=B).unsqueeze(2).to_broadcast([P, B, 4, N // 4]),
        )
        wts["xr"] = (xr_c, xr_s)
        gc_grp = regroup_stationary(gc_raw, 1)
        wts["gb"] = quantise(gb_grp[:].rearrange("p a b c -> p (a b c)"), D, "gb")
        st_transpose(0)
        st_evac(0)
        st_transpose(1)

        bgr = const.tile([P, 4], F32, name="bgr")
        nc.scalar.copy(out=bgr[:], in_=bgr_bf[:])
        nc.scalar.copy(out=besa[:], in_=besa_bf[:])
        bb = const.tile([P, B, N // 2, 2, 4], F32, name="bb")
        gb_c, gb_s = wts["gb"]
        pbs = []
        for h in range(2):
            pb = ps_e.tile([P, 4, P], F32, name="pb", tag="pe")
            for tm in range(4):
                nc.tensor.matmul_mx(
                    out=pb[:, tm, :],
                    lhsT=gb_c[:, P * tm : P * tm + P].bitcast(FP8X4),
                    lhsT_scale=gb_s[:, P * tm : P * tm + P],
                    rhs=x_c[:, P * h : P * h + P].bitcast(FP8X4),
                    rhs_scale=x_s[:, P * h : P * h + P],
                    start=True,
                    stop=True,
                )
            pbs.append(pb)
        ga_grp = regroup_stationary(ga_raw, 2)
        wts["gc"] = quantise(gc_grp[:].rearrange("p a b c -> p (a b c)"), D, "gc")
        st_q1(0)
        wts["ga"] = quantise(ga_grp[:].rearrange("p a b c -> p (a b c)"), D, "ga")
        for b in range(B):
            h, bl = divmod(b, 2)
            nc.vector.tensor_tensor(
                out=bb[:, b].rearrange("p n jh t -> p jh n t"),
                in0=pbs[h][:, :, N * bl : N * bl + N].rearrange("p t (jh n) -> p jh n t", jh=2),
                in1=bgr[:].unsqueeze(1).unsqueeze(1).to_broadcast([P, 2, N // 2, 4]),
                op=ALU.add,
            )
        wts["bb"] = bb[:].rearrange("p b n jh t -> p b (n jh) t")

        we_grp = const.tile([P, F, 4], BF16, name="we_grp", align_bytes=64)

        def regroup_w_esa():
            gps_copy(we_grp[:], we_raw[:].rearrange("p t n -> p n t"))

        def quantise_w_esa():
            wts["we"] = quantise(we_grp[:].rearrange("p n t -> p (n t)"), F, "we")

        go_grp = const.tile([P, 4, P, 4], BF16, name="go_grp", align_bytes=64)
        bgo = const.tile([P, 4], F32, name="bgo")
        nxt = const.tile([P, 4, B * N], F32, name="nxt")
        nxs = {}

        def nx_regroup(piece):
            cols = slice(P // NX_PIECES * piece, P // NX_PIECES * (piece + 1))
            gps_copy(
                go_grp[:, :, cols, :],
                go_raw[:].rearrange("p t (pp tm) -> p tm pp t", tm=4)[:, :, cols, :],
            )

        def nx_quantise():
            wts["go"] = quantise(go_grp[:].rearrange("p a b c -> p (a b c)"), D, "go")

        def nx_matmul():
            go_c, go_s = wts["go"]
            for half in range(2):
                px = ps_tr.tile([P, 2, B * N], F32, name="px", tag="tr")
                for e in range(2):
                    tm = 2 * half + e
                    nc.tensor.matmul_mx(
                        out=px[:, e, :],
                        lhsT=go_c[:, P * tm : P * tm + P].bitcast(FP8X4),
                        lhsT_scale=go_s[:, P * tm : P * tm + P],
                        rhs=x_c[:].bitcast(FP8X4),
                        rhs_scale=x_s[:],
                        start=True,
                        stop=True,
                    )
                nxs[half] = px

        def nx_tanh():
            for tm in range(4):
                nc.scalar.activation(
                    out=nxt[:, tm, :],
                    in_=nxs[tm // 2][:, tm % 2, :],
                    func=ACTF.Tanh,
                    bias=bgo[:, tm : tm + 1],
                    scale=1.0,
                )

        def nx_transpose():
            for r in range(2):
                pt = ps_tr.tile([P, 4, P], F32, name="pt", tag="tr")
                for tm in range(4):
                    nc.tensor.transpose(pt[:, tm, :], nxt[:, tm, P * r : P * r + P], ident[:])
                nxs[r] = pt

        def nx_store():
            for r in range(2):
                nxo = work.tile([P, P, 4], F32, name="nxo", tag="nxo", bufs=2)
                nc.vector.tensor_copy(out=nxo[:], in_=nxs[r][:].rearrange("p tm pp -> p pp tm"))
                nc.sync.dma_start(
                    out=out_0.rearrange("b n d -> (b n) d")[P * r : P * r + P, :],
                    in_=nxo[:].rearrange("p pp tm -> p (pp tm)"),
                )

        def add_then_mx(T, ci):
            if live(T):
                st_add(T, ci)
            Tm, cm = divmod(3 * T + ci + 2, 3)
            if live(Tm):
                st_mx(Tm, cm)

        for T in range(-2, N_TILES):
            early = T < 2
            if live(T - 2):
                st_q2(T - 2)
                st_e(T - 2)
            if live(T + 2) and T + 2 > 0 and not early:
                st_q1(T + 2)
            if live(T - 3):
                st_exp(T - 3)
            if live(T):
                st_direct(T)
            if live(T - 4):
                st_norm(T - 4)
            if live(T):
                st_interleave(T)
            add_then_mx(T, 0)
            if live(T - 3):
                st_q(T - 3)
            add_then_mx(T, 1)
            if live(T + 1):
                st_mx(T + 1, 3)
            if live(T + 2) and T + 2 > 0 and early:
                st_q1(T + 2)
            if live(T - 1):
                for h in range(2):
                    tanh_half(T - 1, h)
            if live(T + 3):
                st_evac_vector(T + 3)
            if live(T - 2):
                st_negmax(T - 2)
            add_then_mx(T, 2)
            if T == 1:
                quantise_w_esa()
            if T == N_TILES - 5:
                nx_quantise()
            if live(T - 5) and (T - 5) % TILES_PER_B == TILES_PER_B - 1:
                copy_sum((T - 5) // TILES_PER_B)
            if live(T + 3):
                st_evac(T + 3)
            if T == 0:
                regroup_w_esa()
                nc.scalar.copy(out=bgo[:], in_=bgo_bf[:])
            if 0 <= T < NX_ROUNDS:
                for piece in range(NX_PIECES // NX_ROUNDS):
                    nx_regroup(NX_PIECES // NX_ROUNDS * T + piece)
            if live(T + 4):
                st_transpose(T + 4)
            if live(T - 4):
                st_accumulate(T - 4)
            if T == N_TILES - 4:
                nx_matmul()
            if T == N_TILES - 3:
                nx_tanh()
                nx_transpose()
            if T == N_TILES - 2:
                nx_store()
                fold_sums(0, last=True)
            if T == N_TILES - 1:
                store_pair(0)

        L = N_TILES - 1
        halves = {}

        def q2_e_half(h):
            if h == 0:
                c2 = work.tile([P, D], U32, name="c2", tag="c2", align_bytes=64)
                s2 = work.tile([P, D], U8, name="s2", tag="s2", align_bytes=64)
                pes[L] = ps_p.tile([P, D], F32, name="pe_last", tag="pp")
                c2s[L] = (c2, s2)
            c2, s2 = c2s[L]
            we_c, we_s = wts["we"]
            cols = slice(4 * N * h, 4 * N * h + 4 * N)
            nc.vector.quantize_mx(
                out=c2[:, cols].bitcast(FP8X4), scales=s2[:, cols], in_=g2s[L][:, 16 * N * h : 16 * N * h + 16 * N]
            )
            nc.tensor.matmul_mx(
                out=pes[L][:, cols],
                lhsT=we_c[:].bitcast(FP8X4),
                lhsT_scale=we_s[:],
                rhs=c2[:, cols].bitcast(FP8X4),
                rhs_scale=s2[:, cols],
                start=True,
                stop=True,
            )

        def negmax_half(h):
            negmax = small.tile([P, 4], F32, name="negmax_half", tag="negmax_half")
            nc.vector.tensor_reduce(
                out=negmax[:],
                in_=pes[L][:, 4 * N * h : 4 * N * h + 4 * N].rearrange("p (j i) -> p j i", j=4),
                axis=AX.X,
                op=ALU.max,
                negate=True,
            )
            halves[h] = [negmax]

        def exp_half(h):
            pexp = work.tile([P, 4, N], F32, name="pexp_half", tag="pexp_half", bufs=2)
            ssum = small.tile([P, 4], F32, name="ssum_half", tag="ssum_half")
            for j in range(4):
                nc.scalar.activation(
                    out=pexp[:, j, :],
                    in_=pes[L][:, N * (4 * h + j) : N * (4 * h + j) + N],
                    func=ACTF.Exp,
                    bias=halves[h][0][:, j : j + 1],
                    scale=1.0,
                    accum_out=ssum[:, j : j + 1],
                )
            halves[h] += [pexp, ssum]

        def q_half(h):
            q = work.tile([P, 4, N], F32, name="q_half", tag="q_half", bufs=2)
            nc.vector.scalar_tensor_tensor(
                out=q[:].rearrange("p j i -> p (j i)"),
                in0=pes[L][:, 4 * N * h : 4 * N * h + 4 * N],
                scalar=besa[:, 0:1],
                in1=halves[h][1][:].rearrange("p j i -> p (j i)"),
                op0=ALU.add,
                op1=ALU.mult,
            )
            rinv = small.tile([P, 4], F32, name="rinv_half", tag="rinv_half")
            nc.vector.reciprocal(out=rinv[:], in_=halves[h][2][:])
            halves[h] += [q, rinv]

        def weigh(eng, T, first, q, rinv):
            count = q[:].shape[1]
            eng.tensor_tensor(
                out=wlast[:, T - GPS_TILES, first : first + count, 1, :],
                in0=q[:],
                in1=rinv[:].unsqueeze(2).to_broadcast([P, count, N]),
                op=ALU.mult,
            )

        def recip(T):
            rinv = small.tile([P, 8], F32, name="rinv", tag="rinv")
            nc.vector.reciprocal(out=rinv[:], in_=exps[T][1][:])
            return rinv

        tanh_half(L, 0)
        tanh_half(L, 1)
        st_q2(L - 1)
        st_e(L - 1)
        q2_e_half(0)
        copy_sum(3)
        st_exp(L - 2)
        weigh(nc.gpsimd, L - 3, 0, qs[L - 3], recip(L - 3))
        q2_e_half(1)
        fold_sums(1, last=False)
        add_transposed(1, wlast[:, 0], last=False)
        st_negmax(L - 1)
        st_exp(L - 1)
        st_q(L - 2)
        weigh(nc.gpsimd, L - 2, 0, qs[L - 2], recip(L - 2))
        negmax_half(0)
        exp_half(0)
        negmax_half(1)
        exp_half(1)
        add_transposed(1, wlast[:, 1], last=False)
        st_q(L - 1)
        r1 = recip(L - 1)
        q_half(0)
        weigh(nc.vector, L - 1, 0, qs[L - 1], r1)
        q_half(1)
        add_transposed(1, wlast[:, 2], last=False)
        weigh(nc.vector, L, 0, halves[0][3], halves[0][4])
        add_transposed(1, wlast[:, 3, 0:4], last=False)
        weigh(nc.vector, L, 4, halves[1][3], halves[1][4])
        add_transposed(1, wlast[:, 3, 4:8], last=True)
        store_pair(1)
